import numpy as np
import ml_dtypes


def mxq(x, axis, fmt="e4m3"):
    dtype, down = {"e4m3": (ml_dtypes.float8_e4m3fn, 7), "e5m2": (ml_dtypes.float8_e5m2, 14)}[fmt]
    v = np.moveaxis(np.asarray(x, np.float32).astype(ml_dtypes.bfloat16).astype(np.float64), axis, -1)
    blocks = v.reshape(v.shape[:-1] + (-1, 32))
    amax = np.abs(blocks).max(-1, keepdims=True)
    byte = np.maximum(np.where(amax > 0, np.frexp(amax)[1] - 1 + 127, 0) - down, 1)
    scale = np.exp2(byte - 127.0)
    codes = (blocks / scale).astype(np.float32).astype(dtype).astype(np.float64)
    return np.moveaxis((codes * scale).reshape(v.shape), -1, axis)


WIDE = False


def mx_kscale(k):
    if not WIDE:
        return np.ones(k)
    levels = np.array([10, -10, 5, -5, 0])
    a = np.random.permutation(np.resize(levels, k // 512 * 4)).reshape(k // 512, 4)
    idx = np.arange(k)
    return np.exp2(a[idx // 512, idx % 128 // 32])


BF16 = ml_dtypes.bfloat16


def bf(x):
    return np.asarray(x, np.float32).astype(BF16)


def f64(x):
    return np.asarray(x).astype(np.float64)


B, S, H, E, V, G, P = 4, 128, 1024, 512, 2048, 5, 3
C = G + P
KNOTS = np.linspace(-1.0 - 2.0 / G * P, 1.0 + 2.0 / G * P, G + 2 * P + 1)


def silu(v):
    e = np.exp(-np.abs(v))
    return v * np.where(v >= 0.0, 1.0, e) / (1.0 + e)


def b_splines(x):
    xe = x[..., None]
    bases = np.where((xe >= KNOTS[:-1]) & (xe < KNOTS[1:]), 1.0, 0.0)
    for p in range(1, P + 1):
        left = (xe - KNOTS[: -(p + 1)]) / (KNOTS[p:-1] - KNOTS[: -(p + 1)])
        right = (KNOTS[p + 1:] - xe) / (KNOTS[p + 1:] - KNOTS[1:-p])
        bases = left * bases[..., :-1] + right * bases[..., 1:]
    return bases


def setup_inputs():
    s = mx_kscale(E)
    u = s / s.min()
    return {"h_norm": bf(np.random.standard_normal((B, S, E)) * u),
            "base_w2": bf(np.random.standard_normal((V, E)) / np.sqrt(E) / u),
            "spline_w2": bf(np.random.standard_normal((V, E, C)) / np.sqrt(E))}


def reference(h_norm, base_w2, spline_w2):
    x = f64(h_norm).reshape(B * S, E)
    base = mxq(silu(x), 1, "e4m3") @ mxq(f64(base_w2), 1, "e4m3").T
    spl = mxq(b_splines(x).reshape(B * S, E * C), 1, "e4m3") @ mxq(f64(spline_w2).reshape(V, E * C), 1, "e4m3").T
    return (base + spl).reshape(B, S, V)

@@ -1,0 +1,259 @@
+import math
+from contextlib import ExitStack
+
+import concourse.mybir as mybir
+from concourse.masks import make_identity
+
+F32 = mybir.dt.float32
+BF16 = mybir.dt.bfloat16
+I32 = mybir.dt.int32
+U32 = mybir.dt.uint32
+U8 = mybir.dt.uint8
+FP8X4 = mybir.dt.float8_e4m3fn_x4
+ACT = mybir.ActivationFunctionType
+ALU = mybir.AluOpType
+
+P = 128
+TOKEN_TILES = 4
+TOKENS = TOKEN_TILES * P
+FEATURES = 512
+OUTPUTS = 2048
+OUT_GROUP = 512
+OUT_GROUPS = OUTPUTS // OUT_GROUP
+ROW_TILES = OUT_GROUP // P
+K_PASS = 512
+WORDS = K_PASS // 2
+SPLINE_PASSES = 8
+BASE_PASS = SPLINE_PASSES
+PASSES = SPLINE_PASSES + 1
+PASS_ORDER = (BASE_PASS, 0, 1, 2, 3, 4, 5, 6, 7)
+HALF_PASSES = 4
+CHUNK = HALF_PASSES * P * 2
+
+X_LIMIT = 4.0
+ROOT_SIXTH = math.sqrt(1.0 / 6.0)
+ROOT_HALF = math.sqrt(0.5)
+
+FLOPS = 2 * TOKENS * OUTPUTS * (FEATURES + 8 * FEATURES)
+
+
+def act_column(tau, k_pass):
+    if k_pass == BASE_PASS:
+        return SPLINE_PASSES * TOKENS + tau * P
+    return (tau * SPLINE_PASSES + k_pass) * P
+
+
+def tile_generatorhead_pb_kernel(tc, h_norm, base_w2, spline_w2, out):
+    nc = tc.nc
+    x_rows = h_norm.rearrange("b s f -> s b f")
+    spline_rows = spline_w2.rearrange("o i c -> o (i c)")
+
+    with ExitStack() as ctx:
+        keep = ctx.enter_context(tc.tile_pool(name="keep", bufs=1))
+        raw_pool = ctx.enter_context(tc.tile_pool(name="raw", bufs=4))
+        grouped_pool = ctx.enter_context(tc.tile_pool(name="grouped", bufs=3))
+        result_pool = ctx.enter_context(tc.tile_pool(name="result", bufs=3))
+        bank_pool = ctx.enter_context(tc.psum_pool(name="bank", bufs=4))
+
+        w_codes = keep.tile([P, PASSES * OUTPUTS], U32, align_bytes=64)
+        w_scales = keep.tile([P, PASSES * OUTPUTS], U8, align_bytes=64)
+        act_codes = keep.tile([P, PASSES * TOKENS], U32, align_bytes=64)
+        act_scales = keep.tile([P, PASSES * TOKENS], U8, align_bytes=64)
+        x_rep = keep.tile([P, SPLINE_PASSES, 2, TOKENS], BF16)
+
+        ident_f32 = keep.tile([P, P], F32)
+        make_identity(nc, ident_f32[:])
+        ident_bf16 = keep.tile([P, P], BF16)
+        make_identity(nc, ident_bf16[:])
+
+        repeat4 = keep.tile([P, 4 * P], BF16)
+        nc.vector.tensor_copy(
+            out=repeat4[:].rearrange("p (f r) -> p f r", r=4),
+            in_=ident_bf16[:].unsqueeze(2).to_broadcast([P, P, 4]),
+        )
+
+        lane = keep.tile([P, 1], I32)
+        nc.gpsimd.iota(out=lane[:], pattern=[[0, 1]], base=0, channel_multiplier=1)
+        lane_mod4 = keep.tile([P, 1], I32)
+        nc.vector.tensor_single_scalar(out=lane_mod4[:], in_=lane[:], scalar=3, op=ALU.bitwise_and)
+        pair = keep.tile([P, 1], F32)
+        nc.vector.tensor_copy(out=pair[:], in_=lane_mod4[:])
+        centre = keep.tile([P, 2], F32)
+        centre_root_half = keep.tile([P, 2], F32)
+        for e in range(2):
+            nc.vector.tensor_scalar(
+                out=centre[:, e : e + 1], in0=pair[:],
+                scalar1=-2.0, scalar2=3.5 - e, op0=ALU.mult, op1=ALU.add,
+            )
+            nc.vector.tensor_scalar(
+                out=centre_root_half[:, e : e + 1], in0=pair[:],
+                scalar1=-2.0 * ROOT_HALF, scalar2=(3.5 - e) * ROOT_HALF, op0=ALU.mult, op1=ALU.add,
+            )
+
+        def transpose_words(bank, words, h):
+            for t in range(2):
+                for u in range(2):
+                    nc.tensor.transpose(
+                        out=bank[:, u, t * P : (t + 1) * P],
+                        in_=words[:, 2 * h + t, u * P : (u + 1) * P],
+                        identity=ident_f32[:],
+                    )
+
+        with tc.tile_pool(name="prep", bufs=1) as prep, tc.psum_pool(name="prep_bank", bufs=4) as prep_bank:
+            x_tok = prep.tile([P, TOKEN_TILES, FEATURES], BF16)
+            nc.sync.dma_start(out=x_tok[:], in_=x_rows)
+
+            silu_grouped = prep.tile([P, 4 * TOKENS], BF16, align_bytes=64)
+            silu_view = silu_grouped[:].rearrange("p (h n u e) -> p h n u e", h=2, u=2, e=2)
+            for h in range(2):
+                bank = prep_bank.tile([P, 2, 2 * P], F32, tag="prep")
+                transpose_words(bank, x_tok[:].bitcast(F32), h)
+                nc.scalar.activation(
+                    out=silu_view[:, h],
+                    in_=bank[:].bitcast(BF16).rearrange("p u (n e) -> p n u e", e=2),
+                    func=ACT.Silu,
+                )
+            base_col = act_column(0, BASE_PASS)
+            nc.vector.quantize_mx(
+                out=act_codes[:, base_col : base_col + TOKENS].bitcast(FP8X4),
+                scales=act_scales[:, base_col : base_col + TOKENS],
+                in_=silu_grouped[:],
+            )
+
+            x_feat = prep.tile([P, FEATURES // P, TOKENS], BF16)
+            for b in range(FEATURES // P):
+                flipped = prep_bank.tile([P, TOKENS], BF16, tag="prep")
+                for tau in range(TOKEN_TILES):
+                    nc.tensor.transpose(
+                        out=flipped[:, tau * P : (tau + 1) * P],
+                        in_=x_tok[:, tau, b * P : (b + 1) * P],
+                        identity=ident_bf16[:],
+                    )
+                nc.vector.tensor_scalar(
+                    out=x_feat[:, b, :], in0=flipped[:],
+                    scalar1=-X_LIMIT, scalar2=X_LIMIT, op0=ALU.max, op1=ALU.min,
+                )
+
+            for g in range(SPLINE_PASSES):
+                spread = prep_bank.tile([P, 2, TOKENS], BF16, tag="prep")
+                for u in range(2):
+                    block = 2 * (g % 2) + u
+                    nc.tensor.matmul(
+                        out=spread[:, u, :],
+                        lhsT=repeat4[:, block * P : (block + 1) * P],
+                        rhs=x_feat[:, g // 2, :],
+                        start=True, stop=True,
+                    )
+                nc.scalar.copy(out=x_rep[:, g], in_=spread[:])
+
+        work = ctx.enter_context(tc.tile_pool(name="work", bufs=1))
+        acc_pool = ctx.enter_context(tc.psum_pool(name="acc", bufs=4))
+
+        def basis_chunk(tau, half):
+            g0 = half * HALF_PASSES
+            x_here = x_rep[:, g0 : g0 + HALF_PASSES, :, tau * P : (tau + 1) * P].rearrange("p g u t -> p g t u")
+            hat = work.tile([P, 2, CHUNK], F32, tag="hat")
+            inner = work.tile([P, 2, CHUNK], F32, tag="inner", bufs=2)
+            for e in range(2):
+                nc.scalar.activation(
+                    out=hat[:, e, :].rearrange("p (g t u) -> p g t u", g=HALF_PASSES, u=2), in_=x_here,
+                    func=ACT.Abs, scale=2.5, bias=centre[:, e : e + 1],
+                )
+            for e in range(2):
+                nc.scalar.activation(
+                    out=inner[:, e, :].rearrange("p (g t u) -> p g t u", g=HALF_PASSES, u=2), in_=x_here,
+                    func=ACT.Square, scale=2.5 * ROOT_HALF, bias=centre_root_half[:, e : e + 1],
+                )
+            nc.vector.tensor_scalar(out=hat[:], in0=hat[:], scalar1=2.0, scalar2=-2.0, op0=ALU.min, op1=ALU.add)
+            outer = work.tile([P, 2, CHUNK], F32, tag="outer")
+            nc.scalar.activation(out=outer[:], in_=hat[:], func=ACT.Square, scale=ROOT_SIXTH)
+            nc.vector.tensor_tensor(out=inner[:], in0=hat[:], in1=inner[:], op=ALU.mult)
+            nc.vector.scalar_tensor_tensor(
+                out=outer[:], in0=hat[:], scalar=-1.0, in1=outer[:], op0=ALU.mult, op1=ALU.mult,
+            )
+            values = work.tile([P, 2 * CHUNK], BF16, tag="values", bufs=2, align_bytes=64)
+            nc.vector.scalar_tensor_tensor(
+                out=values[:].rearrange("p (j e) -> p j e", e=2),
+                in0=inner[:].rearrange("p e j -> p j e"), scalar=2.0 / 3.0,
+                in1=outer[:].rearrange("p e j -> p j e"), op0=ALU.add, op1=ALU.min,
+            )
+            col = act_column(tau, g0)
+            nc.vector.quantize_mx(
+                out=act_codes[:, col : col + HALF_PASSES * P].bitcast(FP8X4),
+                scales=act_scales[:, col : col + HALF_PASSES * P],
+                in_=values[:],
+            )
+
+        def quantise_weight_pass(words, k_pass, og):
+            grouped = grouped_pool.tile([P, 4 * OUT_GROUP], BF16, tag="grouped", align_bytes=64)
+            grouped_words = grouped[:].bitcast(F32).rearrange("p (h n u) -> p h n u", h=2, u=2)
+            for h in range(2):
+                bank = bank_pool.tile([P, 2, 2 * P], F32, tag="bank")
+                transpose_words(bank, words, h)
+                nc.scalar.copy(out=grouped_words[:, h], in_=bank[:].rearrange("p u n -> p n u"))
+            col = k_pass * OUTPUTS + og * OUT_GROUP
+            nc.vector.quantize_mx(
+                out=w_codes[:, col : col + OUT_GROUP].bitcast(FP8X4),
+                scales=w_scales[:, col : col + OUT_GROUP],
+                in_=grouped[:],
+            )
+
+        def weights(og):
+            rows = slice(og * OUT_GROUP, (og + 1) * OUT_GROUP)
+            raw_base = raw_pool.tile([P, ROW_TILES, K_PASS], BF16, tag="raw_base", bufs=2)
+            nc.sync.dma_start(out=raw_base[:], in_=base_w2[rows, :].rearrange("(t p) k -> p t k", p=P))
+            quantise_weight_pass(raw_base[:].bitcast(F32), BASE_PASS, og)
+            for pair_of_passes in range(SPLINE_PASSES // 2):
+                raw = raw_pool.tile([P, ROW_TILES, 2 * K_PASS], BF16, tag="raw")
+                cols = slice(pair_of_passes * 2 * K_PASS, (pair_of_passes + 1) * 2 * K_PASS)
+                nc.sync.dma_start(out=raw[:], in_=spline_rows[rows, cols].rearrange("(t p) k -> p t k", p=P))
+                for q in range(2):
+                    quantise_weight_pass(
+                        raw[:].bitcast(F32)[:, :, q * WORDS : (q + 1) * WORDS], 2 * pair_of_passes + q, og
+                    )
+
+        def multiply(acc, tau, og, passes):
+            for k_pass in passes:
+                a_col = act_column(tau, k_pass)
+                w_col = k_pass * OUTPUTS + og * OUT_GROUP
+                nc.tensor.matmul_mx(
+                    out=acc[:],
+                    lhsT=act_codes[:, a_col : a_col + P].bitcast(FP8X4),
+                    lhsT_scale=act_scales[:, a_col : a_col + P],
+                    rhs=w_codes[:, w_col : w_col + OUT_GROUP].bitcast(FP8X4),
+                    rhs_scale=w_scales[:, w_col : w_col + OUT_GROUP],
+                    start=(k_pass == PASS_ORDER[0]),
+                    stop=(k_pass == PASS_ORDER[-1]),
+                )
+
+        def store(acc, tau, og):
+            result = result_pool.tile([P, OUT_GROUP], F32, tag="result")
+            nc.vector.tensor_copy(out=result[:], in_=acc[:])
+            nc.sync.dma_start(out=out[tau, :, og * OUT_GROUP : (og + 1) * OUT_GROUP], in_=result[:])
+
+        def whole_product(tau, og):
+            acc = acc_pool.tile([P, OUT_GROUP], F32, tag="acc")
+            multiply(acc, tau, og, PASS_ORDER)
+            store(acc, tau, og)
+
+        basis_chunk(0, 0)
+        basis_chunk(0, 1)
+        weights(0)
+        whole_product(0, 0)
+        basis_chunk(1, 0)
+        basis_chunk(1, 1)
+        whole_product(1, 0)
+        for og in range(1, OUT_GROUPS):
+            weights(og)
+            whole_product(0, og)
+            whole_product(1, og)
+
+        for tau in range(2, TOKEN_TILES):
+            accs = [acc_pool.tile([P, OUT_GROUP], F32, name="acc%d" % og, tag="acc") for og in range(OUT_GROUPS)]
+            basis_chunk(tau, 0)
+            for og in range(OUT_GROUPS):
+                multiply(accs[og], tau, og, PASS_ORDER[: 1 + HALF_PASSES])
+            basis_chunk(tau, 1)
+            for og in range(OUT_GROUPS):
+                multiply(accs[og], tau, og, PASS_ORDER[1 + HALF_PASSES :])
+                store(accs[og], tau, og)

@@ -28,7 +28,7 @@ BASE_PASS = SPLINE_PASSES
 PASSES = SPLINE_PASSES + 1
 PASS_ORDER = (BASE_PASS, 0, 1, 2, 3, 4, 5, 6, 7)
 HALF_PASSES = 4
-CHUNK = HALF_PASSES * P * 2
+BANK_PASSES = 2
 
 X_LIMIT = 4.0
 ROOT_SIXTH = math.sqrt(1.0 / 6.0)
@@ -49,17 +49,17 @@ def tile_generatorhead_pb_kernel(tc, h_norm, base_w2, spline_w2, out):
     spline_rows = spline_w2.rearrange("o i c -> o (i c)")
 
     with ExitStack() as ctx:
+        ctx.enter_context(tc.manual_schedule())
         keep = ctx.enter_context(tc.tile_pool(name="keep", bufs=1))
         raw_pool = ctx.enter_context(tc.tile_pool(name="raw", bufs=4))
         grouped_pool = ctx.enter_context(tc.tile_pool(name="grouped", bufs=3))
         result_pool = ctx.enter_context(tc.tile_pool(name="result", bufs=3))
-        bank_pool = ctx.enter_context(tc.psum_pool(name="bank", bufs=4))
 
         w_codes = keep.tile([P, PASSES * OUTPUTS], U32, align_bytes=64)
         w_scales = keep.tile([P, PASSES * OUTPUTS], U8, align_bytes=64)
         act_codes = keep.tile([P, PASSES * TOKENS], U32, align_bytes=64)
         act_scales = keep.tile([P, PASSES * TOKENS], U8, align_bytes=64)
-        x_rep = keep.tile([P, SPLINE_PASSES, 2, TOKENS], BF16)
+        x_rep = keep.tile([P, TOKEN_TILES, 2, SPLINE_PASSES, P], BF16)
 
         ident_f32 = keep.tile([P, P], F32)
         make_identity(nc, ident_f32[:])
@@ -76,19 +76,21 @@ def tile_generatorhead_pb_kernel(tc, h_norm, base_w2, spline_w2, out):
         nc.gpsimd.iota(out=lane[:], pattern=[[0, 1]], base=0, channel_multiplier=1)
         lane_mod4 = keep.tile([P, 1], I32)
         nc.vector.tensor_single_scalar(out=lane_mod4[:], in_=lane[:], scalar=3, op=ALU.bitwise_and)
-        pair = keep.tile([P, 1], F32)
-        nc.vector.tensor_copy(out=pair[:], in_=lane_mod4[:])
-        centre = keep.tile([P, 2], F32)
-        centre_root_half = keep.tile([P, 2], F32)
+        rho = keep.tile([P, 1], F32)
+        nc.vector.tensor_copy(out=rho[:], in_=lane_mod4[:])
+        fold_centre = keep.tile([P, 1], F32)
+        nc.vector.tensor_scalar(out=fold_centre[:], in0=rho[:], scalar1=-1.0, scalar2=1.5, op0=ALU.mult, op1=ALU.add)
+        edge = keep.tile([P, 1], F32)
+        nc.vector.tensor_scalar(out=edge[:], in0=rho[:], scalar1=0.4, scalar2=-0.6, op0=ALU.mult, op1=ALU.add)
+
+        route = keep.tile([P, 2, P], BF16)
         for e in range(2):
-            nc.vector.tensor_scalar(
-                out=centre[:, e : e + 1], in0=pair[:],
-                scalar1=-2.0, scalar2=3.5 - e, op0=ALU.mult, op1=ALU.add,
-            )
-            nc.vector.tensor_scalar(
-                out=centre_root_half[:, e : e + 1], in0=pair[:],
-                scalar1=-2.0 * ROOT_HALF, scalar2=(3.5 - e) * ROOT_HALF, op0=ALU.mult, op1=ALU.add,
-            )
+            for h in range(2):
+                nc.vector.tensor_scalar(
+                    out=route[:, e, :].rearrange("q (i h l) -> q i h l", h=2, l=2)[:, :, h, :],
+                    in0=ident_bf16[:].rearrange("q (i l e) -> q i l e", l=2, e=2)[:, :, :, e],
+                    scalar1=2.0 - 4.0 * h, scalar2=None, op0=ALU.mult,
+                )
 
         def transpose_words(bank, words, h):
             for t in range(2):
@@ -113,12 +115,6 @@ def tile_generatorhead_pb_kernel(tc, h_norm, base_w2, spline_w2, out):
                     in_=bank[:].bitcast(BF16).rearrange("p u (n e) -> p n u e", e=2),
                     func=ACT.Silu,
                 )
-            base_col = act_column(0, BASE_PASS)
-            nc.vector.quantize_mx(
-                out=act_codes[:, base_col : base_col + TOKENS].bitcast(FP8X4),
-                scales=act_scales[:, base_col : base_col + TOKENS],
-                in_=silu_grouped[:],
-            )
 
             x_feat = prep.tile([P, FEATURES // P, TOKENS], BF16)
             for b in range(FEATURES // P):
@@ -144,73 +140,86 @@ def tile_generatorhead_pb_kernel(tc, h_norm, base_w2, spline_w2, out):
                         rhs=x_feat[:, g // 2, :],
                         start=True, stop=True,
                     )
-                nc.scalar.copy(out=x_rep[:, g], in_=spread[:])
+                nc.vector.tensor_copy(out=x_rep[:, :, :, g, :], in_=spread[:].rearrange("p u (a t) -> p a u t", t=P))
 
-        work = ctx.enter_context(tc.tile_pool(name="work", bufs=1))
-        acc_pool = ctx.enter_context(tc.psum_pool(name="acc", bufs=4))
+            base_col = act_column(0, BASE_PASS)
+            nc.vector.quantize_mx(
+                out=act_codes[:, base_col : base_col + TOKENS].bitcast(FP8X4),
+                scales=act_scales[:, base_col : base_col + TOKENS],
+                in_=silu_grouped[:],
+            )
 
-        def basis_chunk(tau, half):
-            g0 = half * HALF_PASSES
-            x_here = x_rep[:, g0 : g0 + HALF_PASSES, :, tau * P : (tau + 1) * P].rearrange("p g u t -> p g t u")
-            hat = work.tile([P, 2, CHUNK], F32, tag="hat")
-            inner = work.tile([P, 2, CHUNK], F32, tag="inner", bufs=2)
-            for e in range(2):
-                nc.scalar.activation(
-                    out=hat[:, e, :].rearrange("p (g t u) -> p g t u", g=HALF_PASSES, u=2), in_=x_here,
-                    func=ACT.Abs, scale=2.5, bias=centre[:, e : e + 1],
-                )
-            for e in range(2):
-                nc.scalar.activation(
-                    out=inner[:, e, :].rearrange("p (g t u) -> p g t u", g=HALF_PASSES, u=2), in_=x_here,
-                    func=ACT.Square, scale=2.5 * ROOT_HALF, bias=centre_root_half[:, e : e + 1],
-                )
+        work = ctx.enter_context(tc.tile_pool(name="work", bufs=2))
+
+        def x_of(chunk):
+            tau, g0, n_passes = chunk
+            return x_rep[:, tau, :, g0 : g0 + n_passes, :].rearrange("p u g t -> p u (g t)")
+
+        def fold(chunk):
+            cols = chunk[2] * P
+            hat = work.tile([P, 2, cols], F32, tag="hat")
+            nc.scalar.activation(out=hat[:], in_=x_of(chunk), func=ACT.Abs, scale=2.5, bias=fold_centre[:])
+            inner = work.tile([P, 2, cols], F32, tag="inner")
+            nc.scalar.activation(out=inner[:], in_=hat[:], func=ACT.Square, scale=ROOT_HALF, bias=-2.0 * ROOT_HALF)
+            nc.scalar.activation(out=hat[:], in_=hat[:], func=ACT.Abs, scale=1.0, bias=-2.0)
+            outer = work.tile([P, 2, cols], F32, tag="outer")
+            nc.scalar.activation(out=outer[:], in_=hat[:], func=ACT.Square, scale=-ROOT_SIXTH, bias=2.0 * ROOT_SIXTH)
+            return hat, inner, outer
+
+        def shape(chunk, folded):
+            cols = chunk[2] * P
+            hat, inner, outer = folded
             nc.vector.tensor_scalar(out=hat[:], in0=hat[:], scalar1=2.0, scalar2=-2.0, op0=ALU.min, op1=ALU.add)
-            outer = work.tile([P, 2, CHUNK], F32, tag="outer")
-            nc.scalar.activation(out=outer[:], in_=hat[:], func=ACT.Square, scale=ROOT_SIXTH)
             nc.vector.tensor_tensor(out=inner[:], in0=hat[:], in1=inner[:], op=ALU.mult)
             nc.vector.scalar_tensor_tensor(
                 out=outer[:], in0=hat[:], scalar=-1.0, in1=outer[:], op0=ALU.mult, op1=ALU.mult,
             )
-            values = work.tile([P, 2 * CHUNK], BF16, tag="values", bufs=2, align_bytes=64)
+            value = work.tile([P, 2, cols], BF16, tag="value")
             nc.vector.scalar_tensor_tensor(
-                out=values[:].rearrange("p (j e) -> p j e", e=2),
-                in0=inner[:].rearrange("p e j -> p j e"), scalar=2.0 / 3.0,
-                in1=outer[:].rearrange("p e j -> p j e"), op0=ALU.add, op1=ALU.min,
+                out=value[:], in0=inner[:], scalar=2.0 / 3.0, in1=outer[:], op0=ALU.add, op1=ALU.min,
             )
+            side = work.tile([P, 2, cols], BF16, tag="side")
+            nc.vector.tensor_scalar(
+                out=side[:], in0=x_of(chunk), scalar1=edge[:], scalar2=0.5, op0=ALU.is_lt, op1=ALU.subtract,
+            )
+            nc.vector.tensor_tensor(out=value[:], in0=value[:], in1=side[:], op=ALU.mult)
+            return value
+
+        def hand_out(chunk, value, route_pool):
+            bank_cols = BANK_PASSES * P
+            banks = []
+            for b in range(chunk[2] // BANK_PASSES):
+                routed = route_pool.tile([P, 4, bank_cols], BF16, name="routed%d" % b, tag="routed")
+                for u in range(2):
+                    for e in range(2):
+                        nc.tensor.matmul(
+                            out=routed[:, 2 * u + e, :],
+                            lhsT=route[:, e, :],
+                            rhs=value[:, u, b * bank_cols : (b + 1) * bank_cols],
+                            start=True, stop=True,
+                        )
+                banks.append(routed)
+            return banks
+
+        def keep_owner(chunk, banks):
+            bank_cols = BANK_PASSES * P
+            values = work.tile([P, 4 * chunk[2] * P], BF16, tag="values", align_bytes=64)
+            for b in range(len(banks)):
+                nc.scalar.activation(
+                    out=values[:, b * 4 * bank_cols : (b + 1) * 4 * bank_cols].rearrange("p (j t) -> p j t", t=4),
+                    in_=banks[b][:].rearrange("p t j -> p j t"),
+                    func=ACT.Relu,
+                )
+            return values
+
+        def quantise_chunk(chunk, values):
+            tau, g0, n_passes = chunk
             col = act_column(tau, g0)
             nc.vector.quantize_mx(
-                out=act_codes[:, col : col + HALF_PASSES * P].bitcast(FP8X4),
-                scales=act_scales[:, col : col + HALF_PASSES * P],
+                out=act_codes[:, col : col + n_passes * P].bitcast(FP8X4),
+                scales=act_scales[:, col : col + n_passes * P],
                 in_=values[:],
             )
-
-        def quantise_weight_pass(words, k_pass, og):
-            grouped = grouped_pool.tile([P, 4 * OUT_GROUP], BF16, tag="grouped", align_bytes=64)
-            grouped_words = grouped[:].bitcast(F32).rearrange("p (h n u) -> p h n u", h=2, u=2)
-            for h in range(2):
-                bank = bank_pool.tile([P, 2, 2 * P], F32, tag="bank")
-                transpose_words(bank, words, h)
-                nc.scalar.copy(out=grouped_words[:, h], in_=bank[:].rearrange("p u n -> p n u"))
-            col = k_pass * OUTPUTS + og * OUT_GROUP
-            nc.vector.quantize_mx(
-                out=w_codes[:, col : col + OUT_GROUP].bitcast(FP8X4),
-                scales=w_scales[:, col : col + OUT_GROUP],
-                in_=grouped[:],
-            )
-
-        def weights(og):
-            rows = slice(og * OUT_GROUP, (og + 1) * OUT_GROUP)
-            raw_base = raw_pool.tile([P, ROW_TILES, K_PASS], BF16, tag="raw_base", bufs=2)
-            nc.sync.dma_start(out=raw_base[:], in_=base_w2[rows, :].rearrange("(t p) k -> p t k", p=P))
-            quantise_weight_pass(raw_base[:].bitcast(F32), BASE_PASS, og)
-            for pair_of_passes in range(SPLINE_PASSES // 2):
-                raw = raw_pool.tile([P, ROW_TILES, 2 * K_PASS], BF16, tag="raw")
-                cols = slice(pair_of_passes * 2 * K_PASS, (pair_of_passes + 1) * 2 * K_PASS)
-                nc.sync.dma_start(out=raw[:], in_=spline_rows[rows, cols].rearrange("(t p) k -> p t k", p=P))
-                for q in range(2):
-                    quantise_weight_pass(
-                        raw[:].bitcast(F32)[:, :, q * WORDS : (q + 1) * WORDS], 2 * pair_of_passes + q, og
-                    )
 
         def multiply(acc, tau, og, passes):
             for k_pass in passes:
@@ -226,34 +235,110 @@ def tile_generatorhead_pb_kernel(tc, h_norm, base_w2, spline_w2, out):
                     stop=(k_pass == PASS_ORDER[-1]),
                 )
 
-        def store(acc, tau, og):
+        def store(acc, tau, og, queue):
             result = result_pool.tile([P, OUT_GROUP], F32, tag="result")
             nc.vector.tensor_copy(out=result[:], in_=acc[:])
-            nc.sync.dma_start(out=out[tau, :, og * OUT_GROUP : (og + 1) * OUT_GROUP], in_=result[:])
+            queue.dma_start(out=out[tau, :, og * OUT_GROUP : (og + 1) * OUT_GROUP], in_=result[:])
 
-        def whole_product(tau, og):
-            acc = acc_pool.tile([P, OUT_GROUP], F32, tag="acc")
-            multiply(acc, tau, og, PASS_ORDER)
-            store(acc, tau, og)
+        def regroup_weight_pass(words, k_pass, bank_pool):
+            grouped = grouped_pool.tile([P, 4 * OUT_GROUP], BF16, tag="grouped", align_bytes=64)
+            grouped_words = grouped[:].bitcast(F32).rearrange("p (h n u) -> p h n u", h=2, u=2)
+            for h in range(2):
+                bank = bank_pool.tile([P, 2, 2 * P], F32, tag="bank")
+                transpose_words(bank, words, h)
+                if h == 1 and k_pass % 3 == 1:
+                    nc.vector.tensor_copy(out=grouped_words[:, h], in_=bank[:].rearrange("p u n -> p n u"))
+                else:
+                    nc.scalar.copy(out=grouped_words[:, h], in_=bank[:].rearrange("p u n -> p n u"))
+            return grouped
 
-        basis_chunk(0, 0)
-        basis_chunk(0, 1)
-        weights(0)
-        whole_product(0, 0)
-        basis_chunk(1, 0)
-        basis_chunk(1, 1)
-        whole_product(1, 0)
-        for og in range(1, OUT_GROUPS):
-            weights(og)
-            whole_product(0, og)
-            whole_product(1, og)
+        def quantise_weight_pass(grouped, k_pass, og):
+            col = k_pass * OUTPUTS + og * OUT_GROUP
+            nc.vector.quantize_mx(
+                out=w_codes[:, col : col + OUT_GROUP].bitcast(FP8X4),
+                scales=w_scales[:, col : col + OUT_GROUP],
+                in_=grouped[:],
+            )
 
-        for tau in range(2, TOKEN_TILES):
-            accs = [acc_pool.tile([P, OUT_GROUP], F32, name="acc%d" % og, tag="acc") for og in range(OUT_GROUPS)]
-            basis_chunk(tau, 0)
-            for og in range(OUT_GROUPS):
-                multiply(accs[og], tau, og, PASS_ORDER[: 1 + HALF_PASSES])
-            basis_chunk(tau, 1)
-            for og in range(OUT_GROUPS):
-                multiply(accs[og], tau, og, PASS_ORDER[1 + HALF_PASSES :])
-                store(accs[og], tau, og)
+        def weights(og, bank_pool, woven):
+            rows = slice(og * OUT_GROUP, (og + 1) * OUT_GROUP)
+            waiting = None
+            for i, k_pass in enumerate(PASS_ORDER):
+                if k_pass == BASE_PASS:
+                    raw = raw_pool.tile([P, ROW_TILES, K_PASS], BF16, tag="raw_base", bufs=2)
+                    nc.sync.dma_start(out=raw[:], in_=base_w2[rows, :].rearrange("(t p) k -> p t k", p=P))
+                elif k_pass % 2 == 0:
+                    raw = raw_pool.tile([P, ROW_TILES, 2 * K_PASS], BF16, tag="raw")
+                    cols = slice(k_pass * K_PASS, (k_pass + 2) * K_PASS)
+                    nc.sync.dma_start(out=raw[:], in_=spline_rows[rows, cols].rearrange("(t p) k -> p t k", p=P))
+                first_word = (k_pass % 2) * WORDS
+                grouped = regroup_weight_pass(raw[:].bitcast(F32)[:, :, first_word : first_word + WORDS], k_pass, bank_pool)
+                if waiting is not None:
+                    quantise_weight_pass(waiting[0], waiting[1], og)
+                waiting = (grouped, k_pass)
+                if i % 3 == 2:
+                    if i == PASSES - 1:
+                        quantise_weight_pass(waiting[0], waiting[1], og)
+                    woven(i // 3)
+
+        chunks = [(tau, g0, HALF_PASSES) for tau in range(TOKEN_TILES - 1) for g0 in (0, HALF_PASSES)]
+        chunks += [(TOKEN_TILES - 1, 0, HALF_PASSES), (TOKEN_TILES - 1, 4, BANK_PASSES), (TOKEN_TILES - 1, 6, BANK_PASSES)]
+
+        with tc.psum_pool(name="bank", bufs=4) as bank_pool, tc.psum_pool(name="routed", bufs=2) as route_pool, tc.psum_pool(name="acc", bufs=2) as acc_pool:
+            folded0 = fold(chunks[0])
+            folded1 = fold(chunks[1])
+            value0 = shape(chunks[0], folded0)
+            tile0_banks = {0: hand_out(chunks[0], value0, route_pool)}
+            value1 = shape(chunks[1], folded1)
+
+            def finish_tile0(i):
+                if i < 2:
+                    values = keep_owner(chunks[i], tile0_banks[i])
+                    if i == 0:
+                        tile0_banks[1] = hand_out(chunks[1], value1, route_pool)
+                    quantise_chunk(chunks[i], values)
+
+            weights(0, bank_pool, finish_tile0)
+
+            tile0_acc = {}
+
+            def tile0_product(og, i):
+                if i == 0:
+                    tile0_acc[og] = acc_pool.tile([P, OUT_GROUP], F32, name="acc_tile0", tag="acc")
+                multiply(tile0_acc[og], 0, og, PASS_ORDER[3 * i : 3 * i + 3])
+                if i == 2:
+                    store(tile0_acc[og], 0, og, nc.gpsimd)
+
+            for og in range(1, OUT_GROUPS):
+                weights(og, bank_pool, lambda i: tile0_product(og - 1, i))
+            first = 2
+            folded = {first: fold(chunks[first])}
+            for i in range(3):
+                tile0_product(OUT_GROUPS - 1, i)
+
+        with tc.psum_pool(name="routed_late", bufs=4) as route_pool, tc.psum_pool(name="acc_late", bufs=4) as acc_pool:
+            last = len(chunks) - 1
+            value = {}
+            banks = {}
+            accs = {}
+            for k in range(first, last + 2):
+                if k + 1 <= last:
+                    folded[k + 1] = fold(chunks[k + 1])
+                if k <= last:
+                    value[k] = shape(chunks[k], folded[k])
+                    banks[k] = hand_out(chunks[k], value[k], route_pool)
+                if k - 1 >= first:
+                    tau, g0, n_passes = chunks[k - 1]
+                    values = keep_owner(chunks[k - 1], banks[k - 1])
+                    quantise_chunk(chunks[k - 1], values)
+                    if g0 == 0:
+                        accs[tau] = [
+                            acc_pool.tile([P, OUT_GROUP], F32, name="acc%d" % og, tag="acc") for og in range(OUT_GROUPS)
+                        ]
+                    passes = list(range(g0, g0 + n_passes))
+                    if g0 == 0:
+                        passes = [BASE_PASS] + passes
+                    for og in range(OUT_GROUPS):
+                        multiply(accs[tau][og], tau, og, passes)
+                        if g0 + n_passes == SPLINE_PASSES:
+                            store(accs[tau][og], tau, og, nc.sync)

@@ -28,7 +28,6 @@ BASE_PASS = SPLINE_PASSES
 PASSES = SPLINE_PASSES + 1
 PASS_ORDER = (BASE_PASS, 0, 1, 2, 3, 4, 5, 6, 7)
 HALF_PASSES = 4
-BANK_PASSES = 2
 
 X_LIMIT = 4.0
 ROOT_SIXTH = math.sqrt(1.0 / 6.0)
@@ -49,17 +48,17 @@ def tile_generatorhead_pb_kernel(tc, h_norm, base_w2, spline_w2, out):
     spline_rows = spline_w2.rearrange("o i c -> o (i c)")
 
     with ExitStack() as ctx:
-        ctx.enter_context(tc.manual_schedule())
         keep = ctx.enter_context(tc.tile_pool(name="keep", bufs=1))
         raw_pool = ctx.enter_context(tc.tile_pool(name="raw", bufs=4))
         grouped_pool = ctx.enter_context(tc.tile_pool(name="grouped", bufs=3))
         result_pool = ctx.enter_context(tc.tile_pool(name="result", bufs=3))
+        bank_pool = ctx.enter_context(tc.psum_pool(name="bank", bufs=4))
 
         w_codes = keep.tile([P, PASSES * OUTPUTS], U32, align_bytes=64)
         w_scales = keep.tile([P, PASSES * OUTPUTS], U8, align_bytes=64)
         act_codes = keep.tile([P, PASSES * TOKENS], U32, align_bytes=64)
         act_scales = keep.tile([P, PASSES * TOKENS], U8, align_bytes=64)
-        x_rep = keep.tile([P, TOKEN_TILES, 2, SPLINE_PASSES, P], BF16)
+        x_rep = keep.tile([P, SPLINE_PASSES, 2, TOKENS], BF16)
 
         ident_f32 = keep.tile([P, P], F32)
         make_identity(nc, ident_f32[:])
@@ -76,21 +75,19 @@ def tile_generatorhead_pb_kernel(tc, h_norm, base_w2, spline_w2, out):
         nc.gpsimd.iota(out=lane[:], pattern=[[0, 1]], base=0, channel_multiplier=1)
         lane_mod4 = keep.tile([P, 1], I32)
         nc.vector.tensor_single_scalar(out=lane_mod4[:], in_=lane[:], scalar=3, op=ALU.bitwise_and)
-        rho = keep.tile([P, 1], F32)
-        nc.vector.tensor_copy(out=rho[:], in_=lane_mod4[:])
-        fold_centre = keep.tile([P, 1], F32)
-        nc.vector.tensor_scalar(out=fold_centre[:], in0=rho[:], scalar1=-1.0, scalar2=1.5, op0=ALU.mult, op1=ALU.add)
-        edge = keep.tile([P, 1], F32)
-        nc.vector.tensor_scalar(out=edge[:], in0=rho[:], scalar1=0.4, scalar2=-0.6, op0=ALU.mult, op1=ALU.add)
-
-        route = keep.tile([P, 2, P], BF16)
+        pair = keep.tile([P, 1], F32)
+        nc.vector.tensor_copy(out=pair[:], in_=lane_mod4[:])
+        centre = keep.tile([P, 2], F32)
+        centre_root_half = keep.tile([P, 2], F32)
         for e in range(2):
-            for h in range(2):
-                nc.vector.tensor_scalar(
-                    out=route[:, e, :].rearrange("q (i h l) -> q i h l", h=2, l=2)[:, :, h, :],
-                    in0=ident_bf16[:].rearrange("q (i l e) -> q i l e", l=2, e=2)[:, :, :, e],
-                    scalar1=2.0 - 4.0 * h, scalar2=None, op0=ALU.mult,
-                )
+            nc.vector.tensor_scalar(
+                out=centre[:, e : e + 1], in0=pair[:],
+                scalar1=-2.0, scalar2=3.5 - e, op0=ALU.mult, op1=ALU.add,
+            )
+            nc.vector.tensor_scalar(
+                out=centre_root_half[:, e : e + 1], in0=pair[:],
+                scalar1=-2.0 * ROOT_HALF, scalar2=(3.5 - e) * ROOT_HALF, op0=ALU.mult, op1=ALU.add,
+            )
 
         def transpose_words(bank, words, h):
             for t in range(2):
@@ -115,6 +112,12 @@ def tile_generatorhead_pb_kernel(tc, h_norm, base_w2, spline_w2, out):
                     in_=bank[:].bitcast(BF16).rearrange("p u (n e) -> p n u e", e=2),
                     func=ACT.Silu,
                 )
+            base_col = act_column(0, BASE_PASS)
+            nc.vector.quantize_mx(
+                out=act_codes[:, base_col : base_col + TOKENS].bitcast(FP8X4),
+                scales=act_scales[:, base_col : base_col + TOKENS],
+                in_=silu_grouped[:],
+            )
 
             x_feat = prep.tile([P, FEATURES // P, TOKENS], BF16)
             for b in range(FEATURES // P):
@@ -140,86 +143,73 @@ def tile_generatorhead_pb_kernel(tc, h_norm, base_w2, spline_w2, out):
                         rhs=x_feat[:, g // 2, :],
                         start=True, stop=True,
                     )
-                nc.vector.tensor_copy(out=x_rep[:, :, :, g, :], in_=spread[:].rearrange("p u (a t) -> p a u t", t=P))
+                nc.vector.tensor_copy(out=x_rep[:, g], in_=spread[:])
 
-            base_col = act_column(0, BASE_PASS)
-            nc.vector.quantize_mx(
-                out=act_codes[:, base_col : base_col + TOKENS].bitcast(FP8X4),
-                scales=act_scales[:, base_col : base_col + TOKENS],
-                in_=silu_grouped[:],
-            )
+        work = ctx.enter_context(tc.tile_pool(name="work", bufs=1))
+        acc_pool = ctx.enter_context(tc.psum_pool(name="acc", bufs=4))
 
-        work = ctx.enter_context(tc.tile_pool(name="work", bufs=2))
-
-        def x_of(chunk):
-            tau, g0, n_passes = chunk
-            return x_rep[:, tau, :, g0 : g0 + n_passes, :].rearrange("p u g t -> p u (g t)")
-
-        def fold(chunk):
-            cols = chunk[2] * P
-            hat = work.tile([P, 2, cols], F32, tag="hat")
-            nc.scalar.activation(out=hat[:], in_=x_of(chunk), func=ACT.Abs, scale=2.5, bias=fold_centre[:])
-            inner = work.tile([P, 2, cols], F32, tag="inner")
-            nc.scalar.activation(out=inner[:], in_=hat[:], func=ACT.Square, scale=ROOT_HALF, bias=-2.0 * ROOT_HALF)
-            nc.scalar.activation(out=hat[:], in_=hat[:], func=ACT.Abs, scale=1.0, bias=-2.0)
-            outer = work.tile([P, 2, cols], F32, tag="outer")
-            nc.scalar.activation(out=outer[:], in_=hat[:], func=ACT.Square, scale=-ROOT_SIXTH, bias=2.0 * ROOT_SIXTH)
-            return hat, inner, outer
-
-        def shape(chunk, folded):
-            cols = chunk[2] * P
-            hat, inner, outer = folded
+        def basis_chunk(tau, g0, n_passes):
+            CHUNK = n_passes * P * 2
+            x_here = x_rep[:, g0 : g0 + n_passes, :, tau * P : (tau + 1) * P].rearrange("p g u t -> p g t u")
+            hat = work.tile([P, 2, CHUNK], F32, tag="hat")
+            inner = work.tile([P, 2, CHUNK], F32, tag="inner", bufs=2)
+            for e in range(2):
+                nc.scalar.activation(
+                    out=hat[:, e, :].rearrange("p (g t u) -> p g t u", g=n_passes, u=2), in_=x_here,
+                    func=ACT.Abs, scale=2.5, bias=centre[:, e : e + 1],
+                )
+            for e in range(2):
+                nc.scalar.activation(
+                    out=inner[:, e, :].rearrange("p (g t u) -> p g t u", g=n_passes, u=2), in_=x_here,
+                    func=ACT.Square, scale=2.5 * ROOT_HALF, bias=centre_root_half[:, e : e + 1],
+                )
             nc.vector.tensor_scalar(out=hat[:], in0=hat[:], scalar1=2.0, scalar2=-2.0, op0=ALU.min, op1=ALU.add)
+            outer = work.tile([P, 2, CHUNK], F32, tag="outer")
+            nc.scalar.activation(out=outer[:], in_=hat[:], func=ACT.Square, scale=ROOT_SIXTH)
             nc.vector.tensor_tensor(out=inner[:], in0=hat[:], in1=inner[:], op=ALU.mult)
             nc.vector.scalar_tensor_tensor(
                 out=outer[:], in0=hat[:], scalar=-1.0, in1=outer[:], op0=ALU.mult, op1=ALU.mult,
             )
-            value = work.tile([P, 2, cols], BF16, tag="value")
+            values = work.tile([P, 2 * CHUNK], BF16, tag="values", bufs=2, align_bytes=64)
             nc.vector.scalar_tensor_tensor(
-                out=value[:], in0=inner[:], scalar=2.0 / 3.0, in1=outer[:], op0=ALU.add, op1=ALU.min,
+                out=values[:].rearrange("p (j e) -> p j e", e=2),
+                in0=inner[:].rearrange("p e j -> p j e"), scalar=2.0 / 3.0,
+                in1=outer[:].rearrange("p e j -> p j e"), op0=ALU.add, op1=ALU.min,
             )
-            side = work.tile([P, 2, cols], BF16, tag="side")
-            nc.vector.tensor_scalar(
-                out=side[:], in0=x_of(chunk), scalar1=edge[:], scalar2=0.5, op0=ALU.is_lt, op1=ALU.subtract,
-            )
-            nc.vector.tensor_tensor(out=value[:], in0=value[:], in1=side[:], op=ALU.mult)
-            return value
-
-        def hand_out(chunk, value, route_pool):
-            bank_cols = BANK_PASSES * P
-            banks = []
-            for b in range(chunk[2] // BANK_PASSES):
-                routed = route_pool.tile([P, 4, bank_cols], BF16, name="routed%d" % b, tag="routed")
-                for u in range(2):
-                    for e in range(2):
-                        nc.tensor.matmul(
-                            out=routed[:, 2 * u + e, :],
-                            lhsT=route[:, e, :],
-                            rhs=value[:, u, b * bank_cols : (b + 1) * bank_cols],
-                            start=True, stop=True,
-                        )
-                banks.append(routed)
-            return banks
-
-        def keep_owner(chunk, banks):
-            bank_cols = BANK_PASSES * P
-            values = work.tile([P, 4 * chunk[2] * P], BF16, tag="values", align_bytes=64)
-            for b in range(len(banks)):
-                nc.scalar.activation(
-                    out=values[:, b * 4 * bank_cols : (b + 1) * 4 * bank_cols].rearrange("p (j t) -> p j t", t=4),
-                    in_=banks[b][:].rearrange("p t j -> p j t"),
-                    func=ACT.Relu,
-                )
-            return values
-
-        def quantise_chunk(chunk, values):
-            tau, g0, n_passes = chunk
             col = act_column(tau, g0)
             nc.vector.quantize_mx(
                 out=act_codes[:, col : col + n_passes * P].bitcast(FP8X4),
                 scales=act_scales[:, col : col + n_passes * P],
                 in_=values[:],
             )
+
+        def quantise_weight_pass(words, k_pass, og):
+            grouped = grouped_pool.tile([P, 4 * OUT_GROUP], BF16, tag="grouped", align_bytes=64)
+            grouped_words = grouped[:].bitcast(F32).rearrange("p (h n u) -> p h n u", h=2, u=2)
+            for h in range(2):
+                bank = bank_pool.tile([P, 2, 2 * P], F32, tag="bank")
+                transpose_words(bank, words, h)
+                nc.scalar.copy(out=grouped_words[:, h], in_=bank[:].rearrange("p u n -> p n u"))
+            col = k_pass * OUTPUTS + og * OUT_GROUP
+            nc.vector.quantize_mx(
+                out=w_codes[:, col : col + OUT_GROUP].bitcast(FP8X4),
+                scales=w_scales[:, col : col + OUT_GROUP],
+                in_=grouped[:],
+            )
+
+        def weights(og):
+            rows = slice(og * OUT_GROUP, (og + 1) * OUT_GROUP)
+            raw_base = raw_pool.tile([P, ROW_TILES, K_PASS], BF16, tag="raw_base", bufs=2)
+            nc.sync.dma_start(out=raw_base[:], in_=base_w2[rows, :].rearrange("(t p) k -> p t k", p=P))
+            quantise_weight_pass(raw_base[:].bitcast(F32), BASE_PASS, og)
+            for pair_of_passes in range(SPLINE_PASSES // 2):
+                raw = raw_pool.tile([P, ROW_TILES, 2 * K_PASS], BF16, tag="raw")
+                cols = slice(pair_of_passes * 2 * K_PASS, (pair_of_passes + 1) * 2 * K_PASS)
+                nc.sync.dma_start(out=raw[:], in_=spline_rows[rows, cols].rearrange("(t p) k -> p t k", p=P))
+                for q in range(2):
+                    quantise_weight_pass(
+                        raw[:].bitcast(F32)[:, :, q * WORDS : (q + 1) * WORDS], 2 * pair_of_passes + q, og
+                    )
 
         def multiply(acc, tau, og, passes):
             for k_pass in passes:
@@ -235,110 +225,38 @@ def tile_generatorhead_pb_kernel(tc, h_norm, base_w2, spline_w2, out):
                     stop=(k_pass == PASS_ORDER[-1]),
                 )
 
-        def store(acc, tau, og, queue):
+        def store(acc, tau, og):
             result = result_pool.tile([P, OUT_GROUP], F32, tag="result")
-            nc.vector.tensor_copy(out=result[:], in_=acc[:])
-            queue.dma_start(out=out[tau, :, og * OUT_GROUP : (og + 1) * OUT_GROUP], in_=result[:])
+            if tau < 2:
+                nc.vector.tensor_copy(out=result[:], in_=acc[:])
+            else:
+                nc.scalar.copy(out=result[:], in_=acc[:])
+            nc.sync.dma_start(out=out[tau, :, og * OUT_GROUP : (og + 1) * OUT_GROUP], in_=result[:])
 
-        def regroup_weight_pass(words, k_pass, bank_pool):
-            grouped = grouped_pool.tile([P, 4 * OUT_GROUP], BF16, tag="grouped", align_bytes=64)
-            grouped_words = grouped[:].bitcast(F32).rearrange("p (h n u) -> p h n u", h=2, u=2)
-            for h in range(2):
-                bank = bank_pool.tile([P, 2, 2 * P], F32, tag="bank")
-                transpose_words(bank, words, h)
-                if h == 1 and k_pass % 3 == 1:
-                    nc.vector.tensor_copy(out=grouped_words[:, h], in_=bank[:].rearrange("p u n -> p n u"))
-                else:
-                    nc.scalar.copy(out=grouped_words[:, h], in_=bank[:].rearrange("p u n -> p n u"))
-            return grouped
+        def whole_product(tau, og):
+            acc = acc_pool.tile([P, OUT_GROUP], F32, tag="acc")
+            multiply(acc, tau, og, PASS_ORDER)
+            store(acc, tau, og)
 
-        def quantise_weight_pass(grouped, k_pass, og):
-            col = k_pass * OUTPUTS + og * OUT_GROUP
-            nc.vector.quantize_mx(
-                out=w_codes[:, col : col + OUT_GROUP].bitcast(FP8X4),
-                scales=w_scales[:, col : col + OUT_GROUP],
-                in_=grouped[:],
-            )
+        basis_chunk(0, 0, HALF_PASSES)
+        basis_chunk(0, HALF_PASSES, HALF_PASSES)
+        weights(0)
+        whole_product(0, 0)
+        basis_chunk(1, 0, HALF_PASSES)
+        basis_chunk(1, HALF_PASSES, HALF_PASSES)
+        whole_product(1, 0)
+        for og in range(1, OUT_GROUPS):
+            weights(og)
+            whole_product(0, og)
+            whole_product(1, og)
 
-        def weights(og, bank_pool, woven):
-            rows = slice(og * OUT_GROUP, (og + 1) * OUT_GROUP)
-            waiting = None
-            for i, k_pass in enumerate(PASS_ORDER):
-                if k_pass == BASE_PASS:
-                    raw = raw_pool.tile([P, ROW_TILES, K_PASS], BF16, tag="raw_base", bufs=2)
-                    nc.sync.dma_start(out=raw[:], in_=base_w2[rows, :].rearrange("(t p) k -> p t k", p=P))
-                elif k_pass % 2 == 0:
-                    raw = raw_pool.tile([P, ROW_TILES, 2 * K_PASS], BF16, tag="raw")
-                    cols = slice(k_pass * K_PASS, (k_pass + 2) * K_PASS)
-                    nc.sync.dma_start(out=raw[:], in_=spline_rows[rows, cols].rearrange("(t p) k -> p t k", p=P))
-                first_word = (k_pass % 2) * WORDS
-                grouped = regroup_weight_pass(raw[:].bitcast(F32)[:, :, first_word : first_word + WORDS], k_pass, bank_pool)
-                if waiting is not None:
-                    quantise_weight_pass(waiting[0], waiting[1], og)
-                waiting = (grouped, k_pass)
-                if i % 3 == 2:
-                    if i == PASSES - 1:
-                        quantise_weight_pass(waiting[0], waiting[1], og)
-                    woven(i // 3)
-
-        chunks = [(tau, g0, HALF_PASSES) for tau in range(TOKEN_TILES - 1) for g0 in (0, HALF_PASSES)]
-        chunks += [(TOKEN_TILES - 1, 0, HALF_PASSES), (TOKEN_TILES - 1, 4, BANK_PASSES), (TOKEN_TILES - 1, 6, BANK_PASSES)]
-
-        with tc.psum_pool(name="bank", bufs=4) as bank_pool, tc.psum_pool(name="routed", bufs=2) as route_pool, tc.psum_pool(name="acc", bufs=2) as acc_pool:
-            folded0 = fold(chunks[0])
-            folded1 = fold(chunks[1])
-            value0 = shape(chunks[0], folded0)
-            tile0_banks = {0: hand_out(chunks[0], value0, route_pool)}
-            value1 = shape(chunks[1], folded1)
-
-            def finish_tile0(i):
-                if i < 2:
-                    values = keep_owner(chunks[i], tile0_banks[i])
-                    if i == 0:
-                        tile0_banks[1] = hand_out(chunks[1], value1, route_pool)
-                    quantise_chunk(chunks[i], values)
-
-            weights(0, bank_pool, finish_tile0)
-
-            tile0_acc = {}
-
-            def tile0_product(og, i):
-                if i == 0:
-                    tile0_acc[og] = acc_pool.tile([P, OUT_GROUP], F32, name="acc_tile0", tag="acc")
-                multiply(tile0_acc[og], 0, og, PASS_ORDER[3 * i : 3 * i + 3])
-                if i == 2:
-                    store(tile0_acc[og], 0, og, nc.gpsimd)
-
-            for og in range(1, OUT_GROUPS):
-                weights(og, bank_pool, lambda i: tile0_product(og - 1, i))
-            first = 2
-            folded = {first: fold(chunks[first])}
-            for i in range(3):
-                tile0_product(OUT_GROUPS - 1, i)
-
-        with tc.psum_pool(name="routed_late", bufs=4) as route_pool, tc.psum_pool(name="acc_late", bufs=4) as acc_pool:
-            last = len(chunks) - 1
-            value = {}
-            banks = {}
-            accs = {}
-            for k in range(first, last + 2):
-                if k + 1 <= last:
-                    folded[k + 1] = fold(chunks[k + 1])
-                if k <= last:
-                    value[k] = shape(chunks[k], folded[k])
-                    banks[k] = hand_out(chunks[k], value[k], route_pool)
-                if k - 1 >= first:
-                    tau, g0, n_passes = chunks[k - 1]
-                    values = keep_owner(chunks[k - 1], banks[k - 1])
-                    quantise_chunk(chunks[k - 1], values)
-                    if g0 == 0:
-                        accs[tau] = [
-                            acc_pool.tile([P, OUT_GROUP], F32, name="acc%d" % og, tag="acc") for og in range(OUT_GROUPS)
-                        ]
-                    passes = list(range(g0, g0 + n_passes))
-                    if g0 == 0:
-                        passes = [BASE_PASS] + passes
-                    for og in range(OUT_GROUPS):
-                        multiply(accs[tau][og], tau, og, passes)
-                        if g0 + n_passes == SPLINE_PASSES:
-                            store(accs[tau][og], tau, og, nc.sync)
+        for tau in range(2, TOKEN_TILES):
+            accs = [acc_pool.tile([P, OUT_GROUP], F32, name="acc%d" % og, tag="acc") for og in range(OUT_GROUPS)]
+            n_passes = HALF_PASSES if tau < TOKEN_TILES - 1 else HALF_PASSES // 2
+            for g0 in range(0, SPLINE_PASSES, n_passes):
+                basis_chunk(tau, g0, n_passes)
+                first = PASS_ORDER.index(g0) if g0 > 0 else 0
+                for og in range(OUT_GROUPS):
+                    multiply(accs[og], tau, og, PASS_ORDER[first : 1 + g0 + n_passes])
+                    if g0 + n_passes == SPLINE_PASSES:
+                        store(accs[og], tau, og)

@@ -28,10 +28,12 @@ BASE_PASS = SPLINE_PASSES
 PASSES = SPLINE_PASSES + 1
 PASS_ORDER = (BASE_PASS, 0, 1, 2, 3, 4, 5, 6, 7)
 HALF_PASSES = 4
+FEATS = K_PASS // 8
 
 X_LIMIT = 4.0
 ROOT_SIXTH = math.sqrt(1.0 / 6.0)
 ROOT_HALF = math.sqrt(0.5)
+ROOT_TWO = math.sqrt(2.0)
 
 FLOPS = 2 * TOKENS * OUTPUTS * (FEATURES + 8 * FEATURES)
 
@@ -52,42 +54,60 @@ def tile_generatorhead_pb_kernel(tc, h_norm, base_w2, spline_w2, out):
         raw_pool = ctx.enter_context(tc.tile_pool(name="raw", bufs=4))
         grouped_pool = ctx.enter_context(tc.tile_pool(name="grouped", bufs=3))
         result_pool = ctx.enter_context(tc.tile_pool(name="result", bufs=3))
-        bank_pool = ctx.enter_context(tc.psum_pool(name="bank", bufs=4))
+        route_pool = ctx.enter_context(tc.psum_pool(name="routed", bufs=2))
 
         w_codes = keep.tile([P, PASSES * OUTPUTS], U32, align_bytes=64)
         w_scales = keep.tile([P, PASSES * OUTPUTS], U8, align_bytes=64)
         act_codes = keep.tile([P, PASSES * TOKENS], U32, align_bytes=64)
         act_scales = keep.tile([P, PASSES * TOKENS], U8, align_bytes=64)
-        x_rep = keep.tile([P, SPLINE_PASSES, 2, TOKENS], BF16)
+        x_rep = keep.tile([P, SPLINE_PASSES, TOKENS], BF16)
 
         ident_f32 = keep.tile([P, P], F32)
         make_identity(nc, ident_f32[:])
         ident_bf16 = keep.tile([P, P], BF16)
         make_identity(nc, ident_bf16[:])
 
-        repeat4 = keep.tile([P, 4 * P], BF16)
+        repeat2 = keep.tile([P, 2 * P], BF16)
         nc.vector.tensor_copy(
-            out=repeat4[:].rearrange("p (f r) -> p f r", r=4),
-            in_=ident_bf16[:].unsqueeze(2).to_broadcast([P, P, 4]),
+            out=repeat2[:].rearrange("p (f b) -> p f b", b=2),
+            in_=ident_bf16[:].unsqueeze(2).to_broadcast([P, P, 2]),
         )
 
         lane = keep.tile([P, 1], I32)
         nc.gpsimd.iota(out=lane[:], pattern=[[0, 1]], base=0, channel_multiplier=1)
-        lane_mod4 = keep.tile([P, 1], I32)
-        nc.vector.tensor_single_scalar(out=lane_mod4[:], in_=lane[:], scalar=3, op=ALU.bitwise_and)
-        pair = keep.tile([P, 1], F32)
-        nc.vector.tensor_copy(out=pair[:], in_=lane_mod4[:])
-        centre = keep.tile([P, 2], F32)
-        centre_root_half = keep.tile([P, 2], F32)
+        lane_mod2 = keep.tile([P, 1], I32)
+        nc.vector.tensor_single_scalar(out=lane_mod2[:], in_=lane[:], scalar=1, op=ALU.bitwise_and)
+        half = keep.tile([P, 1], F32)
+        nc.vector.tensor_copy(out=half[:], in_=lane_mod2[:])
+        z_centre = keep.tile([P, 2], F32)
+        border = keep.tile([P, 2], F32)
         for e in range(2):
             nc.vector.tensor_scalar(
-                out=centre[:, e : e + 1], in0=pair[:],
-                scalar1=-2.0, scalar2=3.5 - e, op0=ALU.mult, op1=ALU.add,
+                out=z_centre[:, e : e + 1], in0=half[:],
+                scalar1=-2.0, scalar2=1.5 - e, op0=ALU.mult, op1=ALU.add,
             )
             nc.vector.tensor_scalar(
-                out=centre_root_half[:, e : e + 1], in0=pair[:],
-                scalar1=-2.0 * ROOT_HALF, scalar2=(3.5 - e) * ROOT_HALF, op0=ALU.mult, op1=ALU.add,
+                out=border[:, e : e + 1], in0=half[:],
+                scalar1=2.0 / 2.5, scalar2=(e - 1.5) / 2.5, op0=ALU.mult, op1=ALU.add,
             )
+
+        two_col = keep.tile([P, 2], F32)
+        nc.vector.tensor_scalar(
+            out=two_col[:, 0:1], in0=half[:], scalar1=0.0, scalar2=-2.0, op0=ALU.mult, op1=ALU.add,
+        )
+        nc.vector.tensor_scalar(
+            out=two_col[:, 1:2], in0=half[:], scalar1=0.0, scalar2=-ROOT_TWO, op0=ALU.mult, op1=ALU.add,
+        )
+
+        route = keep.tile([P, 2, P], BF16)
+        nc.vector.memset(route[:], 0.0)
+        for h in range(2):
+            for g in range(2):
+                nc.vector.tensor_single_scalar(
+                    out=route[:, h, :].rearrange("p (f g b) -> p g f b", g=2, b=2)[:, g],
+                    in_=ident_bf16[:, h * (P // 2) : (h + 1) * (P // 2)].rearrange("p (f b) -> p f b", b=2),
+                    scalar=4.0 * g - 2.0, op=ALU.mult,
+                )
 
         def transpose_words(bank, words, h):
             for t in range(2):
@@ -98,165 +118,194 @@ def tile_generatorhead_pb_kernel(tc, h_norm, base_w2, spline_w2, out):
                         identity=ident_f32[:],
                     )
 
-        with tc.tile_pool(name="prep", bufs=1) as prep, tc.psum_pool(name="prep_bank", bufs=4) as prep_bank:
-            x_tok = prep.tile([P, TOKEN_TILES, FEATURES], BF16)
-            nc.sync.dma_start(out=x_tok[:], in_=x_rows)
+        with tc.psum_pool(name="bank", bufs=3) as bank_pool:
+            with tc.tile_pool(name="prep", bufs=1) as prep, tc.psum_pool(name="prep_bank", bufs=3) as prep_bank:
+                x_tok = prep.tile([P, TOKEN_TILES, FEATURES], BF16)
+                nc.sync.dma_start(out=x_tok[:], in_=x_rows)
 
-            silu_grouped = prep.tile([P, 4 * TOKENS], BF16, align_bytes=64)
-            silu_view = silu_grouped[:].rearrange("p (h n u e) -> p h n u e", h=2, u=2, e=2)
-            for h in range(2):
-                bank = prep_bank.tile([P, 2, 2 * P], F32, tag="prep")
-                transpose_words(bank, x_tok[:].bitcast(F32), h)
-                nc.scalar.activation(
-                    out=silu_view[:, h],
-                    in_=bank[:].bitcast(BF16).rearrange("p u (n e) -> p n u e", e=2),
-                    func=ACT.Silu,
-                )
-            base_col = act_column(0, BASE_PASS)
-            nc.vector.quantize_mx(
-                out=act_codes[:, base_col : base_col + TOKENS].bitcast(FP8X4),
-                scales=act_scales[:, base_col : base_col + TOKENS],
-                in_=silu_grouped[:],
-            )
-
-            x_feat = prep.tile([P, FEATURES // P, TOKENS], BF16)
-            for b in range(FEATURES // P):
-                flipped = prep_bank.tile([P, TOKENS], BF16, tag="prep")
-                for tau in range(TOKEN_TILES):
-                    nc.tensor.transpose(
-                        out=flipped[:, tau * P : (tau + 1) * P],
-                        in_=x_tok[:, tau, b * P : (b + 1) * P],
-                        identity=ident_bf16[:],
+                silu_grouped = prep.tile([P, 4 * TOKENS], BF16, align_bytes=64)
+                silu_view = silu_grouped[:].rearrange("p (h n u e) -> p h n u e", h=2, u=2, e=2)
+                for h in range(2):
+                    bank = prep_bank.tile([P, 2, 2 * P], F32, tag="prep")
+                    transpose_words(bank, x_tok[:].bitcast(F32), h)
+                    nc.scalar.activation(
+                        out=silu_view[:, h],
+                        in_=bank[:].bitcast(BF16).rearrange("p u (n e) -> p n u e", e=2),
+                        func=ACT.Silu,
                     )
-                nc.vector.tensor_scalar(
-                    out=x_feat[:, b, :], in0=flipped[:],
-                    scalar1=-X_LIMIT, scalar2=X_LIMIT, op0=ALU.max, op1=ALU.min,
+                base_col = act_column(0, BASE_PASS)
+                nc.vector.quantize_mx(
+                    out=act_codes[:, base_col : base_col + TOKENS].bitcast(FP8X4),
+                    scales=act_scales[:, base_col : base_col + TOKENS],
+                    in_=silu_grouped[:],
                 )
 
-            for g in range(SPLINE_PASSES):
-                spread = prep_bank.tile([P, 2, TOKENS], BF16, tag="prep")
-                for u in range(2):
-                    block = 2 * (g % 2) + u
-                    nc.tensor.matmul(
-                        out=spread[:, u, :],
-                        lhsT=repeat4[:, block * P : (block + 1) * P],
-                        rhs=x_feat[:, g // 2, :],
-                        start=True, stop=True,
-                    )
-                nc.vector.tensor_copy(out=x_rep[:, g], in_=spread[:])
-
-        work = ctx.enter_context(tc.tile_pool(name="work", bufs=1))
-        acc_pool = ctx.enter_context(tc.psum_pool(name="acc", bufs=4))
-
-        def basis_chunk(tau, g0, n_passes):
-            CHUNK = n_passes * P * 2
-            x_here = x_rep[:, g0 : g0 + n_passes, :, tau * P : (tau + 1) * P].rearrange("p g u t -> p g t u")
-            hat = work.tile([P, 2, CHUNK], F32, tag="hat")
-            inner = work.tile([P, 2, CHUNK], F32, tag="inner", bufs=2)
-            for e in range(2):
-                nc.scalar.activation(
-                    out=hat[:, e, :].rearrange("p (g t u) -> p g t u", g=n_passes, u=2), in_=x_here,
-                    func=ACT.Abs, scale=2.5, bias=centre[:, e : e + 1],
-                )
-            for e in range(2):
-                nc.scalar.activation(
-                    out=inner[:, e, :].rearrange("p (g t u) -> p g t u", g=n_passes, u=2), in_=x_here,
-                    func=ACT.Square, scale=2.5 * ROOT_HALF, bias=centre_root_half[:, e : e + 1],
-                )
-            nc.vector.tensor_scalar(out=hat[:], in0=hat[:], scalar1=2.0, scalar2=-2.0, op0=ALU.min, op1=ALU.add)
-            outer = work.tile([P, 2, CHUNK], F32, tag="outer")
-            nc.scalar.activation(out=outer[:], in_=hat[:], func=ACT.Square, scale=ROOT_SIXTH)
-            nc.vector.tensor_tensor(out=inner[:], in0=hat[:], in1=inner[:], op=ALU.mult)
-            nc.vector.scalar_tensor_tensor(
-                out=outer[:], in0=hat[:], scalar=-1.0, in1=outer[:], op0=ALU.mult, op1=ALU.mult,
-            )
-            values = work.tile([P, 2 * CHUNK], BF16, tag="values", bufs=2, align_bytes=64)
-            nc.vector.scalar_tensor_tensor(
-                out=values[:].rearrange("p (j e) -> p j e", e=2),
-                in0=inner[:].rearrange("p e j -> p j e"), scalar=2.0 / 3.0,
-                in1=outer[:].rearrange("p e j -> p j e"), op0=ALU.add, op1=ALU.min,
-            )
-            col = act_column(tau, g0)
-            nc.vector.quantize_mx(
-                out=act_codes[:, col : col + n_passes * P].bitcast(FP8X4),
-                scales=act_scales[:, col : col + n_passes * P],
-                in_=values[:],
-            )
-
-        def quantise_weight_pass(words, k_pass, og):
-            grouped = grouped_pool.tile([P, 4 * OUT_GROUP], BF16, tag="grouped", align_bytes=64)
-            grouped_words = grouped[:].bitcast(F32).rearrange("p (h n u) -> p h n u", h=2, u=2)
-            for h in range(2):
-                bank = bank_pool.tile([P, 2, 2 * P], F32, tag="bank")
-                transpose_words(bank, words, h)
-                nc.scalar.copy(out=grouped_words[:, h], in_=bank[:].rearrange("p u n -> p n u"))
-            col = k_pass * OUTPUTS + og * OUT_GROUP
-            nc.vector.quantize_mx(
-                out=w_codes[:, col : col + OUT_GROUP].bitcast(FP8X4),
-                scales=w_scales[:, col : col + OUT_GROUP],
-                in_=grouped[:],
-            )
-
-        def weights(og):
-            rows = slice(og * OUT_GROUP, (og + 1) * OUT_GROUP)
-            raw_base = raw_pool.tile([P, ROW_TILES, K_PASS], BF16, tag="raw_base", bufs=2)
-            nc.sync.dma_start(out=raw_base[:], in_=base_w2[rows, :].rearrange("(t p) k -> p t k", p=P))
-            quantise_weight_pass(raw_base[:].bitcast(F32), BASE_PASS, og)
-            for pair_of_passes in range(SPLINE_PASSES // 2):
-                raw = raw_pool.tile([P, ROW_TILES, 2 * K_PASS], BF16, tag="raw")
-                cols = slice(pair_of_passes * 2 * K_PASS, (pair_of_passes + 1) * 2 * K_PASS)
-                nc.sync.dma_start(out=raw[:], in_=spline_rows[rows, cols].rearrange("(t p) k -> p t k", p=P))
-                for q in range(2):
-                    quantise_weight_pass(
-                        raw[:].bitcast(F32)[:, :, q * WORDS : (q + 1) * WORDS], 2 * pair_of_passes + q, og
+                x_feat = prep.tile([P, FEATURES // P, TOKENS], BF16)
+                for b in range(FEATURES // P):
+                    flipped = prep_bank.tile([P, TOKENS], BF16, tag="prep")
+                    for tau in range(TOKEN_TILES):
+                        nc.tensor.transpose(
+                            out=flipped[:, tau * P : (tau + 1) * P],
+                            in_=x_tok[:, tau, b * P : (b + 1) * P],
+                            identity=ident_bf16[:],
+                        )
+                    nc.vector.tensor_scalar(
+                        out=x_feat[:, b, :], in0=flipped[:],
+                        scalar1=-X_LIMIT, scalar2=X_LIMIT, op0=ALU.max, op1=ALU.min,
                     )
 
-        def multiply(acc, tau, og, passes):
-            for k_pass in passes:
-                a_col = act_column(tau, k_pass)
-                w_col = k_pass * OUTPUTS + og * OUT_GROUP
-                nc.tensor.matmul_mx(
-                    out=acc[:],
-                    lhsT=act_codes[:, a_col : a_col + P].bitcast(FP8X4),
-                    lhsT_scale=act_scales[:, a_col : a_col + P],
-                    rhs=w_codes[:, w_col : w_col + OUT_GROUP].bitcast(FP8X4),
-                    rhs_scale=w_scales[:, w_col : w_col + OUT_GROUP],
-                    start=(k_pass == PASS_ORDER[0]),
-                    stop=(k_pass == PASS_ORDER[-1]),
+                for g0 in range(0, SPLINE_PASSES, 2):
+                    spread = prep_bank.tile([P, 2, TOKENS], BF16, tag="prep")
+                    for half_block in range(2):
+                        nc.tensor.matmul(
+                            out=spread[:, half_block, :],
+                            lhsT=repeat2[:, half_block * P : (half_block + 1) * P],
+                            rhs=x_feat[:, g0 // 2, :],
+                            start=True, stop=True,
+                        )
+                    nc.vector.tensor_copy(out=x_rep[:, g0 : g0 + 2], in_=spread[:])
+
+            work = ctx.enter_context(tc.tile_pool(name="work", bufs=2))
+
+            def basis_chunk(tau, g0, n_passes):
+                chunk = n_passes * P
+                x_here = x_rep[:, g0 : g0 + n_passes, tau * P : (tau + 1) * P]
+                away = work.tile([P, 2, chunk], F32, tag="away")
+                for e in range(2):
+                    nc.scalar.activation(
+                        out=away[:, e, :].rearrange("p (g t) -> p g t", t=P), in_=x_here,
+                        func=ACT.Abs, scale=2.5, bias=z_centre[:, e : e + 1],
+                    )
+                minus_two = two_col[:, 0:1]
+                hat = work.tile([P, 2, chunk], F32, tag="hat")
+                nc.scalar.activation(out=hat[:], in_=away[:], func=ACT.Abs, scale=1.0, bias=minus_two)
+                inner = work.tile([P, 2, chunk], F32, tag="inner")
+                nc.scalar.activation(out=inner[:], in_=away[:], func=ACT.Square, scale=ROOT_HALF, bias=two_col[:, 1:2])
+                nc.vector.tensor_scalar(out=hat[:], in0=hat[:], scalar1=2.0, scalar2=-2.0, op0=ALU.min, op1=ALU.add)
+                outer = work.tile([P, 2, chunk], F32, tag="outer")
+                nc.scalar.activation(out=outer[:], in_=hat[:], func=ACT.Square, scale=ROOT_SIXTH)
+                side = work.tile([P, 2, chunk], BF16, tag="side")
+                for e in range(2):
+                    nc.vector.tensor_scalar(
+                        out=side[:, e, :].rearrange("p (g t) -> p g t", t=P), in0=x_here,
+                        scalar1=border[:, e : e + 1], scalar2=0.5, op0=ALU.is_ge, op1=ALU.subtract,
+                    )
+                nc.vector.tensor_tensor(out=inner[:], in0=hat[:], in1=inner[:], op=ALU.mult)
+                nc.vector.scalar_tensor_tensor(
+                    out=outer[:], in0=hat[:], scalar=-1.0, in1=outer[:], op0=ALU.mult, op1=ALU.mult,
+                )
+                signed = work.tile([P, 2, chunk], BF16, tag="signed")
+                nc.vector.scalar_tensor_tensor(
+                    out=signed[:], in0=inner[:], scalar=2.0 / 3.0, in1=outer[:], op0=ALU.add, op1=ALU.min,
+                )
+                nc.vector.tensor_tensor(out=signed[:], in0=signed[:], in1=side[:], op=ALU.mult)
+                values = work.tile([P, n_passes, P, 2, 2], BF16, tag="values", align_bytes=64)
+                for pair in range(n_passes // 2):
+                    routed = route_pool.tile([P, 2, 2, P, 2], BF16, tag="routed")
+                    for h in range(2):
+                        nc.tensor.matmul(
+                            out=routed[:, h],
+                            lhsT=route[:, h, :],
+                            rhs=signed[:, :, pair * 2 * P : (pair + 1) * 2 * P].rearrange("p e (g t) -> p g t e", t=P),
+                            start=True, stop=True,
+                        )
+                    for q in range(2):
+                        nc.vector.tensor_single_scalar(
+                            out=values[:, 2 * pair + q], in_=routed[:, :, q].rearrange("p h t e -> p t h e"),
+                            scalar=0.0, op=ALU.max,
+                        )
+                col = act_column(tau, g0)
+                nc.vector.quantize_mx(
+                    out=act_codes[:, col : col + n_passes * P].bitcast(FP8X4),
+                    scales=act_scales[:, col : col + n_passes * P],
+                    in_=values[:].rearrange("p g t h e -> p (g t h e)"),
                 )
 
-        def store(acc, tau, og):
-            result = result_pool.tile([P, OUT_GROUP], F32, tag="result")
-            if tau < 2:
-                nc.vector.tensor_copy(out=result[:], in_=acc[:])
-            else:
-                nc.scalar.copy(out=result[:], in_=acc[:])
-            nc.sync.dma_start(out=out[tau, :, og * OUT_GROUP : (og + 1) * OUT_GROUP], in_=result[:])
+            def quantise_weight_pass(words, k_pass, og):
+                grouped = grouped_pool.tile([P, 4 * OUT_GROUP], BF16, tag="grouped", align_bytes=64)
+                grouped_words = grouped[:].bitcast(F32).rearrange("p (h n u) -> p h n u", h=2, u=2)
+                for h in range(2):
+                    bank = bank_pool.tile([P, 2, 2 * P], F32, tag="bank")
+                    transpose_words(bank, words, h)
+                    nc.scalar.copy(out=grouped_words[:, h], in_=bank[:].rearrange("p u n -> p n u"))
+                col = k_pass * OUTPUTS + og * OUT_GROUP
+                nc.vector.quantize_mx(
+                    out=w_codes[:, col : col + OUT_GROUP].bitcast(FP8X4),
+                    scales=w_scales[:, col : col + OUT_GROUP],
+                    in_=grouped[:],
+                )
 
-        def whole_product(tau, og):
-            acc = acc_pool.tile([P, OUT_GROUP], F32, tag="acc")
-            multiply(acc, tau, og, PASS_ORDER)
-            store(acc, tau, og)
+            def weights(og):
+                rows = slice(og * OUT_GROUP, (og + 1) * OUT_GROUP)
+                raw_base = raw_pool.tile([P, ROW_TILES, K_PASS], BF16, tag="raw_base", bufs=2)
+                nc.sync.dma_start(out=raw_base[:], in_=base_w2[rows, :].rearrange("(t p) k -> p t k", p=P))
+                quantise_weight_pass(raw_base[:].bitcast(F32), BASE_PASS, og)
+                for pair_of_passes in range(SPLINE_PASSES // 2):
+                    raw = raw_pool.tile([P, ROW_TILES, 2 * K_PASS], BF16, tag="raw")
+                    cols = slice(pair_of_passes * 2 * K_PASS, (pair_of_passes + 1) * 2 * K_PASS)
+                    nc.sync.dma_start(out=raw[:], in_=spline_rows[rows, cols].rearrange("(t p) k -> p t k", p=P))
+                    for q in range(2):
+                        quantise_weight_pass(
+                            raw[:].bitcast(F32)[:, :, q * WORDS : (q + 1) * WORDS], 2 * pair_of_passes + q, og
+                        )
 
-        basis_chunk(0, 0, HALF_PASSES)
-        basis_chunk(0, HALF_PASSES, HALF_PASSES)
-        weights(0)
-        whole_product(0, 0)
-        basis_chunk(1, 0, HALF_PASSES)
-        basis_chunk(1, HALF_PASSES, HALF_PASSES)
-        whole_product(1, 0)
-        for og in range(1, OUT_GROUPS):
-            weights(og)
-            whole_product(0, og)
-            whole_product(1, og)
+            def multiply(acc, tau, og, passes):
+                for k_pass in passes:
+                    a_col = act_column(tau, k_pass)
+                    w_col = k_pass * OUTPUTS + og * OUT_GROUP
+                    nc.tensor.matmul_mx(
+                        out=acc[:],
+                        lhsT=act_codes[:, a_col : a_col + P].bitcast(FP8X4),
+                        lhsT_scale=act_scales[:, a_col : a_col + P],
+                        rhs=w_codes[:, w_col : w_col + OUT_GROUP].bitcast(FP8X4),
+                        rhs_scale=w_scales[:, w_col : w_col + OUT_GROUP],
+                        start=(k_pass == PASS_ORDER[0]),
+                        stop=(k_pass == PASS_ORDER[-1]),
+                    )
 
-        for tau in range(2, TOKEN_TILES):
-            accs = [acc_pool.tile([P, OUT_GROUP], F32, name="acc%d" % og, tag="acc") for og in range(OUT_GROUPS)]
-            n_passes = HALF_PASSES if tau < TOKEN_TILES - 1 else HALF_PASSES // 2
-            for g0 in range(0, SPLINE_PASSES, n_passes):
-                basis_chunk(tau, g0, n_passes)
-                first = PASS_ORDER.index(g0) if g0 > 0 else 0
-                for og in range(OUT_GROUPS):
-                    multiply(accs[og], tau, og, PASS_ORDER[first : 1 + g0 + n_passes])
-                    if g0 + n_passes == SPLINE_PASSES:
-                        store(accs[og], tau, og)
+            def store(acc, tau, og):
+                result = result_pool.tile([P, OUT_GROUP], F32, tag="result")
+                if og % 2 == 0:
+                    nc.vector.tensor_copy(out=result[:], in_=acc[:])
+                else:
+                    nc.scalar.copy(out=result[:], in_=acc[:])
+                nc.sync.dma_start(out=out[tau, :, og * OUT_GROUP : (og + 1) * OUT_GROUP], in_=result[:])
+
+            def basis(tau):
+                for g0 in range(0, SPLINE_PASSES, HALF_PASSES):
+                    basis_chunk(tau, g0, HALF_PASSES)
+
+            with tc.psum_pool(name="acc", bufs=3) as acc_pool:
+
+                def products(taus, og):
+                    for tau in taus:
+                        acc = acc_pool.tile([P, OUT_GROUP], F32, tag="acc")
+                        multiply(acc, tau, og, PASS_ORDER)
+                        store(acc, tau, og)
+
+                basis(0)
+                weights(0)
+                products((0,), 0)
+                basis(1)
+                products((1,), 0)
+                weights(1)
+                products((0, 1), 1)
+                basis(2)
+                products((2,), 0)
+                products((2,), 1)
+                weights(2)
+                products((0, 1, 2), 2)
+                weights(3)
+                products((0, 1, 2), 3)
+
+        tail_pool = ctx.enter_context(tc.psum_pool(name="tail", bufs=4))
+        tau = TOKEN_TILES - 1
+        accs = [tail_pool.tile([P, OUT_GROUP], F32, name="acc%d" % og, tag="tail") for og in range(OUT_GROUPS)]
+        n_passes = HALF_PASSES // 2
+        for g0 in range(0, SPLINE_PASSES, n_passes):
+            basis_chunk(tau, g0, n_passes)
+            first = PASS_ORDER.index(g0) if g0 > 0 else 0
+            for og in range(OUT_GROUPS):
+                multiply(accs[og], tau, og, PASS_ORDER[first : 1 + g0 + n_passes])
+                if g0 + n_passes == SPLINE_PASSES:
+                    store(accs[og], tau, og)

@@ -184,19 +184,20 @@ def tile_generatorhead_pb_kernel(tc, h_norm, base_w2, spline_w2, out):
                 nc.vector.tensor_scalar(out=hat[:], in0=hat[:], scalar1=2.0, scalar2=-2.0, op0=ALU.min, op1=ALU.add)
                 outer = work.tile([P, 2, chunk], F32, tag="outer")
                 nc.scalar.activation(out=outer[:], in_=hat[:], func=ACT.Square, scale=ROOT_SIXTH)
-                side = work.tile([P, 2, chunk], BF16, tag="side")
+                side = work.tile([P, chunk, 2], BF16, tag="side")
                 for e in range(2):
                     nc.vector.tensor_scalar(
-                        out=side[:, e, :].rearrange("p (g t) -> p g t", t=P), in0=x_here,
+                        out=side[:, :, e].rearrange("p (g t) -> p g t", t=P), in0=x_here,
                         scalar1=border[:, e : e + 1], scalar2=0.5, op0=ALU.is_ge, op1=ALU.subtract,
                     )
                 nc.vector.tensor_tensor(out=inner[:], in0=hat[:], in1=inner[:], op=ALU.mult)
                 nc.vector.scalar_tensor_tensor(
                     out=outer[:], in0=hat[:], scalar=-1.0, in1=outer[:], op0=ALU.mult, op1=ALU.mult,
                 )
-                signed = work.tile([P, 2, chunk], BF16, tag="signed")
+                signed = work.tile([P, chunk, 2], BF16, tag="signed")
                 nc.vector.scalar_tensor_tensor(
-                    out=signed[:], in0=inner[:], scalar=2.0 / 3.0, in1=outer[:], op0=ALU.add, op1=ALU.min,
+                    out=signed[:], in0=inner[:].rearrange("p e j -> p j e"), scalar=2.0 / 3.0,
+                    in1=outer[:].rearrange("p e j -> p j e"), op0=ALU.add, op1=ALU.min,
                 )
                 nc.vector.tensor_tensor(out=signed[:], in0=signed[:], in1=side[:], op=ALU.mult)
                 values = work.tile([P, n_passes, P, 2, 2], BF16, tag="values", align_bytes=64)
@@ -204,9 +205,9 @@ def tile_generatorhead_pb_kernel(tc, h_norm, base_w2, spline_w2, out):
                     routed = route_pool.tile([P, 2, 2, P, 2], BF16, tag="routed")
                     for h in range(2):
                         nc.tensor.matmul(
-                            out=routed[:, h],
+                            out=routed[:, h].rearrange("p g t e -> p (g t e)"),
                             lhsT=route[:, h, :],
-                            rhs=signed[:, :, pair * 2 * P : (pair + 1) * 2 * P].rearrange("p e (g t) -> p g t e", t=P),
+                            rhs=signed[:, pair * 2 * P : (pair + 1) * 2 * P, :].rearrange("p j e -> p (j e)"),
                             start=True, stop=True,
                         )
                     for q in range(2):

@@ -60,18 +60,19 @@ def tile_generatorhead_pb_kernel(tc, h_norm, base_w2, spline_w2, out):
         w_scales = keep.tile([P, PASSES * OUTPUTS], U8, align_bytes=64)
         act_codes = keep.tile([P, PASSES * TOKENS], U32, align_bytes=64)
         act_scales = keep.tile([P, PASSES * TOKENS], U8, align_bytes=64)
-        x_rep = keep.tile([P, SPLINE_PASSES, TOKENS], BF16)
+        x_rep = keep.tile([P, SPLINE_PASSES // 2, 2, TOKENS], BF16)
 
         ident_f32 = keep.tile([P, P], F32)
         make_identity(nc, ident_f32[:])
         ident_bf16 = keep.tile([P, P], BF16)
         make_identity(nc, ident_bf16[:])
 
-        repeat2 = keep.tile([P, 2 * P], BF16)
-        nc.vector.tensor_copy(
-            out=repeat2[:].rearrange("p (f b) -> p f b", b=2),
-            in_=ident_bf16[:].unsqueeze(2).to_broadcast([P, P, 2]),
-        )
+        repeat2 = keep.tile([P, 2, P], BF16)
+        for u in range(2):
+            nc.vector.tensor_copy(
+                out=repeat2[:, u, :].rearrange("p (r f b) -> p r f b", r=2, b=2),
+                in_=ident_bf16[:].rearrange("p (r u f) -> p u r f", r=2, u=2)[:, u].unsqueeze(3).to_broadcast([P, 2, 32, 2]),
+            )
 
         lane = keep.tile([P, 1], I32)
         nc.gpsimd.iota(out=lane[:], pattern=[[0, 1]], base=0, channel_multiplier=1)
@@ -154,26 +155,24 @@ def tile_generatorhead_pb_kernel(tc, h_norm, base_w2, spline_w2, out):
                         scalar1=-X_LIMIT, scalar2=X_LIMIT, op0=ALU.max, op1=ALU.min,
                     )
 
-                for g0 in range(0, SPLINE_PASSES, 2):
+                for pair in range(SPLINE_PASSES // 2):
                     spread = prep_bank.tile([P, 2, TOKENS], BF16, tag="prep")
-                    for half_block in range(2):
+                    for u in range(2):
                         nc.tensor.matmul(
-                            out=spread[:, half_block, :],
-                            lhsT=repeat2[:, half_block * P : (half_block + 1) * P],
-                            rhs=x_feat[:, g0 // 2, :],
+                            out=spread[:, u, :], lhsT=repeat2[:, u, :], rhs=x_feat[:, pair, :],
                             start=True, stop=True,
                         )
-                    nc.vector.tensor_copy(out=x_rep[:, g0 : g0 + 2], in_=spread[:])
+                    nc.vector.tensor_copy(out=x_rep[:, pair], in_=spread[:])
 
             work = ctx.enter_context(tc.tile_pool(name="work", bufs=2))
 
             def basis_chunk(tau, g0, n_passes):
                 chunk = n_passes * P
-                x_here = x_rep[:, g0 : g0 + n_passes, tau * P : (tau + 1) * P]
+                x_here = x_rep[:, g0 // 2 : (g0 + n_passes) // 2, :, tau * P : (tau + 1) * P].rearrange("p g u t -> p g t u")
                 away = work.tile([P, 2, chunk], F32, tag="away")
                 for e in range(2):
                     nc.scalar.activation(
-                        out=away[:, e, :].rearrange("p (g t) -> p g t", t=P), in_=x_here,
+                        out=away[:, e, :].rearrange("p (g t u) -> p g t u", t=P, u=2), in_=x_here,
                         func=ACT.Abs, scale=2.5, bias=z_centre[:, e : e + 1],
                     )
                 minus_two = two_col[:, 0:1]
@@ -187,7 +186,7 @@ def tile_generatorhead_pb_kernel(tc, h_norm, base_w2, spline_w2, out):
                 side = work.tile([P, chunk, 2], BF16, tag="side")
                 for e in range(2):
                     nc.vector.tensor_scalar(
-                        out=side[:, :, e].rearrange("p (g t) -> p g t", t=P), in0=x_here,
+                        out=side[:, :, e].rearrange("p (g t u) -> p g t u", t=P, u=2), in0=x_here,
                         scalar1=border[:, e : e + 1], scalar2=0.5, op0=ALU.is_ge, op1=ALU.subtract,
                     )
                 nc.vector.tensor_tensor(out=inner[:], in0=hat[:], in1=inner[:], op=ALU.mult)
@@ -200,26 +199,25 @@ def tile_generatorhead_pb_kernel(tc, h_norm, base_w2, spline_w2, out):
                     in1=outer[:].rearrange("p e j -> p j e"), op0=ALU.add, op1=ALU.min,
                 )
                 nc.vector.tensor_tensor(out=signed[:], in0=signed[:], in1=side[:], op=ALU.mult)
-                values = work.tile([P, n_passes, P, 2, 2], BF16, tag="values", align_bytes=64)
+                values = work.tile([P, n_passes * 4 * P], BF16, tag="values", align_bytes=64)
                 for pair in range(n_passes // 2):
-                    routed = route_pool.tile([P, 2, 2, P, 2], BF16, tag="routed")
-                    for h in range(2):
+                    routed = route_pool.tile([P, 2, 4 * P], BF16, tag="routed")
+                    for r in range(2):
                         nc.tensor.matmul(
-                            out=routed[:, h].rearrange("p g t e -> p (g t e)"),
-                            lhsT=route[:, h, :],
+                            out=routed[:, r, :],
+                            lhsT=route[:, r, :],
                             rhs=signed[:, pair * 2 * P : (pair + 1) * 2 * P, :].rearrange("p j e -> p (j e)"),
                             start=True, stop=True,
                         )
-                    for q in range(2):
-                        nc.vector.tensor_single_scalar(
-                            out=values[:, 2 * pair + q], in_=routed[:, :, q].rearrange("p h t e -> p t h e"),
-                            scalar=0.0, op=ALU.max,
-                        )
+                    nc.vector.tensor_single_scalar(
+                        out=values[:, pair * 8 * P : (pair + 1) * 8 * P], in_=routed[:].rearrange("p r j -> p (r j)"),
+                        scalar=0.0, op=ALU.max,
+                    )
                 col = act_column(tau, g0)
                 nc.vector.quantize_mx(
                     out=act_codes[:, col : col + n_passes * P].bitcast(FP8X4),
                     scales=act_scales[:, col : col + n_passes * P],
-                    in_=values[:].rearrange("p g t h e -> p (g t h e)"),
+                    in_=values[:],
                 )
 
             def quantise_weight_pass(words, k_pass, og):

@@ -54,7 +54,7 @@ def tile_generatorhead_pb_kernel(tc, h_norm, base_w2, spline_w2, out):
         raw_pool = ctx.enter_context(tc.tile_pool(name="raw", bufs=4))
         grouped_pool = ctx.enter_context(tc.tile_pool(name="grouped", bufs=3))
         result_pool = ctx.enter_context(tc.tile_pool(name="result", bufs=3))
-        route_pool = ctx.enter_context(tc.psum_pool(name="routed", bufs=2))
+        route_pool = ctx.enter_context(tc.psum_pool(name="routed", bufs=1))
 
         w_codes = keep.tile([P, PASSES * OUTPUTS], U32, align_bytes=64)
         w_scales = keep.tile([P, PASSES * OUTPUTS], U8, align_bytes=64)
@@ -119,7 +119,7 @@ def tile_generatorhead_pb_kernel(tc, h_norm, base_w2, spline_w2, out):
                         identity=ident_f32[:],
                     )
 
-        with tc.psum_pool(name="bank", bufs=3) as bank_pool:
+        with tc.psum_pool(name="bank", bufs=4) as bank_pool:
             with tc.tile_pool(name="prep", bufs=1) as prep, tc.psum_pool(name="prep_bank", bufs=3) as prep_bank:
                 x_tok = prep.tile([P, TOKEN_TILES, FEATURES], BF16)
                 nc.sync.dma_start(out=x_tok[:], in_=x_rows)
@@ -234,12 +234,13 @@ def tile_generatorhead_pb_kernel(tc, h_norm, base_w2, spline_w2, out):
                     in_=grouped[:],
                 )
 
-            def weights(og):
+            def weights(og, half):
                 rows = slice(og * OUT_GROUP, (og + 1) * OUT_GROUP)
-                raw_base = raw_pool.tile([P, ROW_TILES, K_PASS], BF16, tag="raw_base", bufs=2)
-                nc.sync.dma_start(out=raw_base[:], in_=base_w2[rows, :].rearrange("(t p) k -> p t k", p=P))
-                quantise_weight_pass(raw_base[:].bitcast(F32), BASE_PASS, og)
-                for pair_of_passes in range(SPLINE_PASSES // 2):
+                if half == 0:
+                    raw_base = raw_pool.tile([P, ROW_TILES, K_PASS], BF16, tag="raw_base", bufs=2)
+                    nc.sync.dma_start(out=raw_base[:], in_=base_w2[rows, :].rearrange("(t p) k -> p t k", p=P))
+                    quantise_weight_pass(raw_base[:].bitcast(F32), BASE_PASS, og)
+                for pair_of_passes in range(half * HALF_PASSES // 2, (half + 1) * HALF_PASSES // 2):
                     raw = raw_pool.tile([P, ROW_TILES, 2 * K_PASS], BF16, tag="raw")
                     cols = slice(pair_of_passes * 2 * K_PASS, (pair_of_passes + 1) * 2 * K_PASS)
                     nc.sync.dma_start(out=raw[:], in_=spline_rows[rows, cols].rearrange("(t p) k -> p t k", p=P))
@@ -270,41 +271,19 @@ def tile_generatorhead_pb_kernel(tc, h_norm, base_w2, spline_w2, out):
                     nc.scalar.copy(out=result[:], in_=acc[:])
                 nc.sync.dma_start(out=out[tau, :, og * OUT_GROUP : (og + 1) * OUT_GROUP], in_=result[:])
 
-            def basis(tau):
-                for g0 in range(0, SPLINE_PASSES, HALF_PASSES):
-                    basis_chunk(tau, g0, HALF_PASSES)
-
             with tc.psum_pool(name="acc", bufs=3) as acc_pool:
 
-                def products(taus, og):
-                    for tau in taus:
-                        acc = acc_pool.tile([P, OUT_GROUP], F32, tag="acc")
-                        multiply(acc, tau, og, PASS_ORDER)
-                        store(acc, tau, og)
+                def product(tau, og):
+                    acc = acc_pool.tile([P, OUT_GROUP], F32, tag="acc")
+                    multiply(acc, tau, og, PASS_ORDER)
+                    store(acc, tau, og)
 
-                basis(0)
-                weights(0)
-                products((0,), 0)
-                basis(1)
-                products((1,), 0)
-                weights(1)
-                products((0, 1), 1)
-                basis(2)
-                products((2,), 0)
-                products((2,), 1)
-                weights(2)
-                products((0, 1, 2), 2)
-                weights(3)
-                products((0, 1, 2), 3)
-
-        tail_pool = ctx.enter_context(tc.psum_pool(name="tail", bufs=4))
-        tau = TOKEN_TILES - 1
-        accs = [tail_pool.tile([P, OUT_GROUP], F32, name="acc%d" % og, tag="tail") for og in range(OUT_GROUPS)]
-        n_passes = HALF_PASSES // 2
-        for g0 in range(0, SPLINE_PASSES, n_passes):
-            basis_chunk(tau, g0, n_passes)
-            first = PASS_ORDER.index(g0) if g0 > 0 else 0
-            for og in range(OUT_GROUPS):
-                multiply(accs[og], tau, og, PASS_ORDER[first : 1 + g0 + n_passes])
-                if g0 + n_passes == SPLINE_PASSES:
-                    store(accs[og], tau, og)
+                for step in range(2 * TOKEN_TILES):
+                    last, half = divmod(step, 2)
+                    weights(last, half)
+                    basis_chunk(last, half * HALF_PASSES, HALF_PASSES)
+                    if half == 1:
+                        for other in range(last):
+                            product(last, other)
+                            product(other, last)
+                        product(last, last)

@@ -28,7 +28,7 @@ BASE_PASS = SPLINE_PASSES
 PASSES = SPLINE_PASSES + 1
 PASS_ORDER = (BASE_PASS, 0, 1, 2, 3, 4, 5, 6, 7)
 HALF_PASSES = 4
-FEATS = K_PASS // 8
+PASSES_BETWEEN = 4
 
 X_LIMIT = 4.0
 ROOT_SIXTH = math.sqrt(1.0 / 6.0)
@@ -67,19 +67,14 @@ def tile_generatorhead_pb_kernel(tc, h_norm, base_w2, spline_w2, out):
         ident_bf16 = keep.tile([P, P], BF16)
         make_identity(nc, ident_bf16[:])
 
-        repeat2 = keep.tile([P, 2, P], BF16)
-        for u in range(2):
-            nc.vector.tensor_copy(
-                out=repeat2[:, u, :].rearrange("p (r f b) -> p r f b", r=2, b=2),
-                in_=ident_bf16[:].rearrange("p (r u f) -> p u r f", r=2, u=2)[:, u].unsqueeze(3).to_broadcast([P, 2, 32, 2]),
-            )
-
         lane = keep.tile([P, 1], I32)
         nc.gpsimd.iota(out=lane[:], pattern=[[0, 1]], base=0, channel_multiplier=1)
         lane_mod2 = keep.tile([P, 1], I32)
-        nc.vector.tensor_single_scalar(out=lane_mod2[:], in_=lane[:], scalar=1, op=ALU.bitwise_and)
+        nc.vector.tensor_single_scalar(out=lane_mod2[:], in_=lane[:], scalar=32, op=ALU.bitwise_and)
+        half32 = keep.tile([P, 1], F32)
+        nc.vector.tensor_copy(out=half32[:], in_=lane_mod2[:])
         half = keep.tile([P, 1], F32)
-        nc.vector.tensor_copy(out=half[:], in_=lane_mod2[:])
+        nc.vector.tensor_single_scalar(out=half[:], in_=half32[:], scalar=1.0 / 32.0, op=ALU.mult)
         z_centre = keep.tile([P, 2], F32)
         border = keep.tile([P, 2], F32)
         for e in range(2):
@@ -106,7 +101,7 @@ def tile_generatorhead_pb_kernel(tc, h_norm, base_w2, spline_w2, out):
             for g in range(2):
                 nc.vector.tensor_single_scalar(
                     out=route[:, h, :].rearrange("p (f g b) -> p g f b", g=2, b=2)[:, g],
-                    in_=ident_bf16[:, h * (P // 2) : (h + 1) * (P // 2)].rearrange("p (f b) -> p f b", b=2),
+                    in_=ident_bf16[:, h * (P // 2) : (h + 1) * (P // 2)].rearrange("p (b f) -> p f b", b=2),
                     scalar=4.0 * g - 2.0, op=ALU.mult,
                 )
 
@@ -120,11 +115,11 @@ def tile_generatorhead_pb_kernel(tc, h_norm, base_w2, spline_w2, out):
                     )
 
         with tc.psum_pool(name="bank", bufs=4) as bank_pool:
-            with tc.tile_pool(name="prep", bufs=1) as prep, tc.psum_pool(name="prep_bank", bufs=3) as prep_bank:
-                x_tok = prep.tile([P, TOKEN_TILES, FEATURES], BF16)
+            with tc.psum_pool(name="prep_bank", bufs=3) as prep_bank:
+                x_tok = raw_pool.tile([P, TOKEN_TILES, FEATURES], BF16, tag="raw_base", bufs=2)
                 nc.sync.dma_start(out=x_tok[:], in_=x_rows)
 
-                silu_grouped = prep.tile([P, 4 * TOKENS], BF16, align_bytes=64)
+                silu_grouped = grouped_pool.tile([P, 4 * TOKENS], BF16, tag="grouped", align_bytes=64)
                 silu_view = silu_grouped[:].rearrange("p (h n u e) -> p h n u e", h=2, u=2, e=2)
                 for h in range(2):
                     bank = prep_bank.tile([P, 2, 2 * P], F32, tag="prep")
@@ -134,35 +129,33 @@ def tile_generatorhead_pb_kernel(tc, h_norm, base_w2, spline_w2, out):
                         in_=bank[:].bitcast(BF16).rearrange("p u (n e) -> p n u e", e=2),
                         func=ACT.Silu,
                     )
+                x_twice = raw_pool.tile([P, TOKEN_TILES * FEATURES // P, 2, P], BF16, tag="raw")
+                x_split = x_tok[:].rearrange("p t (G r u f) -> p u (t G) r f", r=2, u=2, f=32)
+                twice_split = x_twice[:].rearrange("p j u (r b f) -> p u b j r f", r=2, b=2)
+                for u in range(2):
+                    for b in range(2):
+                        nc.vector.tensor_scalar(
+                            out=twice_split[:, u, b], in0=x_split[:, u],
+                            scalar1=-X_LIMIT, scalar2=X_LIMIT, op0=ALU.max, op1=ALU.min,
+                        )
+
+                for pair in range(SPLINE_PASSES // 2):
+                    flipped = prep_bank.tile([P, 2, TOKENS], BF16, tag="prep")
+                    for u in range(2):
+                        for tau in range(TOKEN_TILES):
+                            nc.tensor.transpose(
+                                out=flipped[:, u, tau * P : (tau + 1) * P],
+                                in_=x_twice[:, tau * (FEATURES // P) + pair, u, :],
+                                identity=ident_bf16[:],
+                            )
+                    nc.vector.tensor_copy(out=x_rep[:, pair], in_=flipped[:])
+
                 base_col = act_column(0, BASE_PASS)
                 nc.vector.quantize_mx(
                     out=act_codes[:, base_col : base_col + TOKENS].bitcast(FP8X4),
                     scales=act_scales[:, base_col : base_col + TOKENS],
                     in_=silu_grouped[:],
                 )
-
-                x_feat = prep.tile([P, FEATURES // P, TOKENS], BF16)
-                for b in range(FEATURES // P):
-                    flipped = prep_bank.tile([P, TOKENS], BF16, tag="prep")
-                    for tau in range(TOKEN_TILES):
-                        nc.tensor.transpose(
-                            out=flipped[:, tau * P : (tau + 1) * P],
-                            in_=x_tok[:, tau, b * P : (b + 1) * P],
-                            identity=ident_bf16[:],
-                        )
-                    nc.vector.tensor_scalar(
-                        out=x_feat[:, b, :], in0=flipped[:],
-                        scalar1=-X_LIMIT, scalar2=X_LIMIT, op0=ALU.max, op1=ALU.min,
-                    )
-
-                for pair in range(SPLINE_PASSES // 2):
-                    spread = prep_bank.tile([P, 2, TOKENS], BF16, tag="prep")
-                    for u in range(2):
-                        nc.tensor.matmul(
-                            out=spread[:, u, :], lhsT=repeat2[:, u, :], rhs=x_feat[:, pair, :],
-                            start=True, stop=True,
-                        )
-                    nc.vector.tensor_copy(out=x_rep[:, pair], in_=spread[:])
 
             work = ctx.enter_context(tc.tile_pool(name="work", bufs=2))
 
@@ -234,12 +227,13 @@ def tile_generatorhead_pb_kernel(tc, h_norm, base_w2, spline_w2, out):
                     in_=grouped[:],
                 )
 
-            def weights(og, half):
+            def weights(og, half, advance):
                 rows = slice(og * OUT_GROUP, (og + 1) * OUT_GROUP)
                 if half == 0:
                     raw_base = raw_pool.tile([P, ROW_TILES, K_PASS], BF16, tag="raw_base", bufs=2)
                     nc.sync.dma_start(out=raw_base[:], in_=base_w2[rows, :].rearrange("(t p) k -> p t k", p=P))
                     quantise_weight_pass(raw_base[:].bitcast(F32), BASE_PASS, og)
+                    advance(PASSES_BETWEEN)
                 for pair_of_passes in range(half * HALF_PASSES // 2, (half + 1) * HALF_PASSES // 2):
                     raw = raw_pool.tile([P, ROW_TILES, 2 * K_PASS], BF16, tag="raw")
                     cols = slice(pair_of_passes * 2 * K_PASS, (pair_of_passes + 1) * 2 * K_PASS)
@@ -248,6 +242,7 @@ def tile_generatorhead_pb_kernel(tc, h_norm, base_w2, spline_w2, out):
                         quantise_weight_pass(
                             raw[:].bitcast(F32)[:, :, q * WORDS : (q + 1) * WORDS], 2 * pair_of_passes + q, og
                         )
+                        advance(PASSES_BETWEEN)
 
             def multiply(acc, tau, og, passes):
                 for k_pass in passes:
@@ -273,17 +268,31 @@ def tile_generatorhead_pb_kernel(tc, h_norm, base_w2, spline_w2, out):
 
             with tc.psum_pool(name="acc", bufs=3) as acc_pool:
 
-                def product(tau, og):
-                    acc = acc_pool.tile([P, OUT_GROUP], F32, tag="acc")
-                    multiply(acc, tau, og, PASS_ORDER)
-                    store(acc, tau, og)
+                ready = []
+                begun = []
+                passes_done = []
+
+                def advance(passes):
+                    for turn in range(passes):
+                        if len(passes_done) == 0:
+                            if len(begun) == len(ready):
+                                return
+                            acc = acc_pool.tile([P, OUT_GROUP], F32, tag="acc")
+                            begun.append(acc)
+                        tau, og = ready[len(begun) - 1]
+                        position = len(passes_done)
+                        multiply(begun[-1], tau, og, PASS_ORDER[position : position + 1])
+                        passes_done.append(turn)
+                        if len(passes_done) == PASSES:
+                            store(begun[-1], tau, og)
+                            passes_done.clear()
 
                 for step in range(2 * TOKEN_TILES):
                     last, half = divmod(step, 2)
-                    weights(last, half)
+                    weights(last, half, advance)
                     basis_chunk(last, half * HALF_PASSES, HALF_PASSES)
                     if half == 1:
                         for other in range(last):
-                            product(last, other)
-                            product(other, last)
-                        product(last, last)
+                            ready.extend([(last, other), (other, last)])
+                        ready.extend([(last, last)])
+                advance(PASSES * len(ready))

@@ -28,7 +28,8 @@ BASE_PASS = SPLINE_PASSES
 PASSES = SPLINE_PASSES + 1
 PASS_ORDER = (BASE_PASS, 0, 1, 2, 3, 4, 5, 6, 7)
 HALF_PASSES = 4
-PASSES_BETWEEN = 4
+PASSES_BETWEEN = 5
+DELIVERY_AFTER = 2
 
 X_LIMIT = 4.0
 ROOT_SIXTH = math.sqrt(1.0 / 6.0)
@@ -53,7 +54,7 @@ def tile_generatorhead_pb_kernel(tc, h_norm, base_w2, spline_w2, out):
         keep = ctx.enter_context(tc.tile_pool(name="keep", bufs=1))
         raw_pool = ctx.enter_context(tc.tile_pool(name="raw", bufs=4))
         grouped_pool = ctx.enter_context(tc.tile_pool(name="grouped", bufs=3))
-        result_pool = ctx.enter_context(tc.tile_pool(name="result", bufs=3))
+        result_pool = ctx.enter_context(tc.tile_pool(name="result", bufs=5))
         route_pool = ctx.enter_context(tc.psum_pool(name="routed", bufs=1))
 
         w_codes = keep.tile([P, PASSES * OUTPUTS], U32, align_bytes=64)
@@ -159,7 +160,7 @@ def tile_generatorhead_pb_kernel(tc, h_norm, base_w2, spline_w2, out):
 
             work = ctx.enter_context(tc.tile_pool(name="work", bufs=2))
 
-            def basis_chunk(tau, g0, n_passes):
+            def evaluate_chunk(tau, g0, n_passes):
                 chunk = n_passes * P
                 x_here = x_rep[:, g0 // 2 : (g0 + n_passes) // 2, :, tau * P : (tau + 1) * P].rearrange("p g u t -> p g t u")
                 away = work.tile([P, 2, chunk], F32, tag="away")
@@ -192,6 +193,9 @@ def tile_generatorhead_pb_kernel(tc, h_norm, base_w2, spline_w2, out):
                     in1=outer[:].rearrange("p e j -> p j e"), op0=ALU.add, op1=ALU.min,
                 )
                 nc.vector.tensor_tensor(out=signed[:], in0=signed[:], in1=side[:], op=ALU.mult)
+                return signed
+
+            def deliver_chunk(signed, tau, g0, n_passes):
                 values = work.tile([P, n_passes * 4 * P], BF16, tag="values", align_bytes=64)
                 for pair in range(n_passes // 2):
                     routed = route_pool.tile([P, 2, 4 * P], BF16, tag="routed")
@@ -219,7 +223,10 @@ def tile_generatorhead_pb_kernel(tc, h_norm, base_w2, spline_w2, out):
                 for h in range(2):
                     bank = bank_pool.tile([P, 2, 2 * P], F32, tag="bank")
                     transpose_words(bank, words, h)
-                    nc.scalar.copy(out=grouped_words[:, h], in_=bank[:].rearrange("p u n -> p n u"))
+                    if og == 0 and k_pass in PASS_ORDER[: 1 + HALF_PASSES] and h == 1:
+                        nc.vector.tensor_copy(out=grouped_words[:, h], in_=bank[:].rearrange("p u n -> p n u"))
+                    else:
+                        nc.scalar.copy(out=grouped_words[:, h], in_=bank[:].rearrange("p u n -> p n u"))
                 col = k_pass * OUTPUTS + og * OUT_GROUP
                 nc.vector.quantize_mx(
                     out=w_codes[:, col : col + OUT_GROUP].bitcast(FP8X4),
@@ -227,13 +234,13 @@ def tile_generatorhead_pb_kernel(tc, h_norm, base_w2, spline_w2, out):
                     in_=grouped[:],
                 )
 
-            def weights(og, half, advance):
+            def weights(og, half, after_a_pass):
                 rows = slice(og * OUT_GROUP, (og + 1) * OUT_GROUP)
                 if half == 0:
                     raw_base = raw_pool.tile([P, ROW_TILES, K_PASS], BF16, tag="raw_base", bufs=2)
                     nc.sync.dma_start(out=raw_base[:], in_=base_w2[rows, :].rearrange("(t p) k -> p t k", p=P))
                     quantise_weight_pass(raw_base[:].bitcast(F32), BASE_PASS, og)
-                    advance(PASSES_BETWEEN)
+                    after_a_pass()
                 for pair_of_passes in range(half * HALF_PASSES // 2, (half + 1) * HALF_PASSES // 2):
                     raw = raw_pool.tile([P, ROW_TILES, 2 * K_PASS], BF16, tag="raw")
                     cols = slice(pair_of_passes * 2 * K_PASS, (pair_of_passes + 1) * 2 * K_PASS)
@@ -242,7 +249,7 @@ def tile_generatorhead_pb_kernel(tc, h_norm, base_w2, spline_w2, out):
                         quantise_weight_pass(
                             raw[:].bitcast(F32)[:, :, q * WORDS : (q + 1) * WORDS], 2 * pair_of_passes + q, og
                         )
-                        advance(PASSES_BETWEEN)
+                        after_a_pass()
 
             def multiply(acc, tau, og, passes):
                 for k_pass in passes:
@@ -287,12 +294,30 @@ def tile_generatorhead_pb_kernel(tc, h_norm, base_w2, spline_w2, out):
                             store(begun[-1], tau, og)
                             passes_done.clear()
 
+                evaluated = []
+                turns = []
+
+                def deliver():
+                    for chunk in evaluated:
+                        deliver_chunk(*chunk)
+                        tau, half = chunk[1], chunk[2] // HALF_PASSES
+                        if half == 1:
+                            for other in range(tau):
+                                ready.extend([(tau, other), (other, tau)])
+                            ready.extend([(tau, tau)])
+                    evaluated.clear()
+
+                def after_a_weight_pass():
+                    turns.append(1)
+                    if len(turns) == DELIVERY_AFTER:
+                        deliver()
+                    advance(PASSES_BETWEEN)
+
                 for step in range(2 * TOKEN_TILES):
                     last, half = divmod(step, 2)
-                    weights(last, half, advance)
-                    basis_chunk(last, half * HALF_PASSES, HALF_PASSES)
-                    if half == 1:
-                        for other in range(last):
-                            ready.extend([(last, other), (other, last)])
-                        ready.extend([(last, last)])
+                    weights(last, half, after_a_weight_pass)
+                    signed = evaluate_chunk(last, half * HALF_PASSES, HALF_PASSES)
+                    evaluated.append((signed, last, half * HALF_PASSES, HALF_PASSES))
+                    turns.clear()
+                deliver()
                 advance(PASSES * len(ready))

@@ -26,9 +26,10 @@ WORDS = K_PASS // 2
 SPLINE_PASSES = 8
 BASE_PASS = SPLINE_PASSES
 PASSES = SPLINE_PASSES + 1
-PASS_ORDER = (BASE_PASS, 0, 1, 2, 3, 4, 5, 6, 7)
+PASS_ORDER = (0, 1, 2, 3, 4, 5, 6, 7, BASE_PASS)
 HALF_PASSES = 4
 PASSES_BETWEEN = 5
+HALVES = (PASS_ORDER[:HALF_PASSES], PASS_ORDER[HALF_PASSES:])
 DELIVERY_AFTER = 2
 
 X_LIMIT = 4.0
@@ -54,7 +55,7 @@ def tile_generatorhead_pb_kernel(tc, h_norm, base_w2, spline_w2, out):
         keep = ctx.enter_context(tc.tile_pool(name="keep", bufs=1))
         raw_pool = ctx.enter_context(tc.tile_pool(name="raw", bufs=4))
         grouped_pool = ctx.enter_context(tc.tile_pool(name="grouped", bufs=3))
-        result_pool = ctx.enter_context(tc.tile_pool(name="result", bufs=5))
+        result_pool = ctx.enter_context(tc.tile_pool(name="result", bufs=3))
         route_pool = ctx.enter_context(tc.psum_pool(name="routed", bufs=1))
 
         w_codes = keep.tile([P, PASSES * OUTPUTS], U32, align_bytes=64)
@@ -106,6 +107,17 @@ def tile_generatorhead_pb_kernel(tc, h_norm, base_w2, spline_w2, out):
                     scalar=4.0 * g - 2.0, op=ALU.mult,
                 )
 
+        def load_base(og):
+            blocks = raw_pool.tile([P, OUT_GROUP // 16, 64], BF16, tag="raw_base", bufs=OUT_GROUPS, align_bytes=64)
+            rows = base_w2[og * OUT_GROUP : (og + 1) * OUT_GROUP, :]
+            for q in range(4):
+                for u in range(2):
+                    nc.gpsimd.dma_start(
+                        out=blocks[32 * q + u : 32 * (q + 1) : 2],
+                        in_=rows[:, 64 * (4 * u + q) : 64 * (4 * u + q + 1)].rearrange("(j o) k -> o j k", o=16),
+                    )
+            return blocks
+
         def transpose_words(bank, words, h):
             for t in range(2):
                 for u in range(2):
@@ -117,8 +129,9 @@ def tile_generatorhead_pb_kernel(tc, h_norm, base_w2, spline_w2, out):
 
         with tc.psum_pool(name="bank", bufs=4) as bank_pool:
             with tc.psum_pool(name="prep_bank", bufs=3) as prep_bank:
-                x_tok = raw_pool.tile([P, TOKEN_TILES, FEATURES], BF16, tag="raw_base", bufs=2)
+                x_tok = raw_pool.tile([P, TOKEN_TILES, FEATURES], BF16, tag="raw")
                 nc.sync.dma_start(out=x_tok[:], in_=x_rows)
+                raw_base = [load_base(og) for og in range(OUT_GROUPS)]
 
                 silu_grouped = grouped_pool.tile([P, 4 * TOKENS], BF16, tag="grouped", align_bytes=64)
                 silu_view = silu_grouped[:].rearrange("p (h n u e) -> p h n u e", h=2, u=2, e=2)
@@ -223,10 +236,13 @@ def tile_generatorhead_pb_kernel(tc, h_norm, base_w2, spline_w2, out):
                 for h in range(2):
                     bank = bank_pool.tile([P, 2, 2 * P], F32, tag="bank")
                     transpose_words(bank, words, h)
-                    if og == 0 and k_pass in PASS_ORDER[: 1 + HALF_PASSES] and h == 1:
+                    if og == 0 and k_pass < HALF_PASSES and h == 1:
                         nc.vector.tensor_copy(out=grouped_words[:, h], in_=bank[:].rearrange("p u n -> p n u"))
                     else:
                         nc.scalar.copy(out=grouped_words[:, h], in_=bank[:].rearrange("p u n -> p n u"))
+                quantise_grouped(grouped, k_pass, og)
+
+            def quantise_grouped(grouped, k_pass, og):
                 col = k_pass * OUTPUTS + og * OUT_GROUP
                 nc.vector.quantize_mx(
                     out=w_codes[:, col : col + OUT_GROUP].bitcast(FP8X4),
@@ -234,13 +250,16 @@ def tile_generatorhead_pb_kernel(tc, h_norm, base_w2, spline_w2, out):
                     in_=grouped[:],
                 )
 
+            def quantise_base_pass(og):
+                grouped = grouped_pool.tile([P, 4 * OUT_GROUP], BF16, tag="grouped", align_bytes=64)
+                nc.vector.transpose(
+                    out=grouped[:].bitcast(F32),
+                    in_=raw_base[og][:].rearrange("p j k -> p (j k)").bitcast(F32),
+                )
+                quantise_grouped(grouped, BASE_PASS, og)
+
             def weights(og, half, after_a_pass):
                 rows = slice(og * OUT_GROUP, (og + 1) * OUT_GROUP)
-                if half == 0:
-                    raw_base = raw_pool.tile([P, ROW_TILES, K_PASS], BF16, tag="raw_base", bufs=2)
-                    nc.sync.dma_start(out=raw_base[:], in_=base_w2[rows, :].rearrange("(t p) k -> p t k", p=P))
-                    quantise_weight_pass(raw_base[:].bitcast(F32), BASE_PASS, og)
-                    after_a_pass()
                 for pair_of_passes in range(half * HALF_PASSES // 2, (half + 1) * HALF_PASSES // 2):
                     raw = raw_pool.tile([P, ROW_TILES, 2 * K_PASS], BF16, tag="raw")
                     cols = slice(pair_of_passes * 2 * K_PASS, (pair_of_passes + 1) * 2 * K_PASS)
@@ -250,6 +269,9 @@ def tile_generatorhead_pb_kernel(tc, h_norm, base_w2, spline_w2, out):
                             raw[:].bitcast(F32)[:, :, q * WORDS : (q + 1) * WORDS], 2 * pair_of_passes + q, og
                         )
                         after_a_pass()
+                if half == 1:
+                    quantise_base_pass(og)
+                    after_a_pass()
 
             def multiply(acc, tau, og, passes):
                 for k_pass in passes:
@@ -267,57 +289,56 @@ def tile_generatorhead_pb_kernel(tc, h_norm, base_w2, spline_w2, out):
 
             def store(acc, tau, og):
                 result = result_pool.tile([P, OUT_GROUP], F32, tag="result")
-                if og % 2 == 0:
-                    nc.vector.tensor_copy(out=result[:], in_=acc[:])
-                else:
-                    nc.scalar.copy(out=result[:], in_=acc[:])
+                nc.scalar.copy(out=result[:], in_=acc[:])
                 nc.sync.dma_start(out=out[tau, :, og * OUT_GROUP : (og + 1) * OUT_GROUP], in_=result[:])
 
+            accs = {}
+            ready = []
+            begun = []
+            evaluated = []
+            turns = []
+
+            def advance(pool, passes):
+                for tau, og, k_pass in ready[len(begun) : len(begun) + passes]:
+                    if k_pass == PASS_ORDER[0]:
+                        acc = pool.tile([P, OUT_GROUP], F32, tag="acc")
+                        accs[tau, og] = acc
+                    multiply(accs[tau, og], tau, og, (k_pass,))
+                    begun.append(k_pass)
+                    if k_pass == PASS_ORDER[-1]:
+                        store(accs[tau, og], tau, og)
+
+            def deliver():
+                for chunk in evaluated:
+                    deliver_chunk(*chunk)
+                    tau, half = chunk[1], chunk[2] // HALF_PASSES
+                    if half == 1 and tau < TOKEN_TILES - 1:
+                        for og in range(tau + 1):
+                            ready.extend([(tau, og, k_pass) for k_pass in PASS_ORDER])
+                evaluated.clear()
+
             with tc.psum_pool(name="acc", bufs=3) as acc_pool:
-
-                ready = []
-                begun = []
-                passes_done = []
-
-                def advance(passes):
-                    for turn in range(passes):
-                        if len(passes_done) == 0:
-                            if len(begun) == len(ready):
-                                return
-                            acc = acc_pool.tile([P, OUT_GROUP], F32, tag="acc")
-                            begun.append(acc)
-                        tau, og = ready[len(begun) - 1]
-                        position = len(passes_done)
-                        multiply(begun[-1], tau, og, PASS_ORDER[position : position + 1])
-                        passes_done.append(turn)
-                        if len(passes_done) == PASSES:
-                            store(begun[-1], tau, og)
-                            passes_done.clear()
-
-                evaluated = []
-                turns = []
-
-                def deliver():
-                    for chunk in evaluated:
-                        deliver_chunk(*chunk)
-                        tau, half = chunk[1], chunk[2] // HALF_PASSES
-                        if half == 1:
-                            for other in range(tau):
-                                ready.extend([(tau, other), (other, tau)])
-                            ready.extend([(tau, tau)])
-                    evaluated.clear()
 
                 def after_a_weight_pass():
                     turns.append(1)
                     if len(turns) == DELIVERY_AFTER:
                         deliver()
-                    advance(PASSES_BETWEEN)
+                    advance(acc_pool, PASSES_BETWEEN)
 
                 for step in range(2 * TOKEN_TILES):
                     last, half = divmod(step, 2)
                     weights(last, half, after_a_weight_pass)
+                    for tau in range(last):
+                        ready.extend([(tau, last, k_pass) for k_pass in HALVES[half]])
                     signed = evaluate_chunk(last, half * HALF_PASSES, HALF_PASSES)
                     evaluated.append((signed, last, half * HALF_PASSES, HALF_PASSES))
                     turns.clear()
                 deliver()
-                advance(PASSES * len(ready))
+                advance(acc_pool, len(ready))
+
+        tail_pool = ctx.enter_context(tc.psum_pool(name="tail", bufs=4))
+        tau = TOKEN_TILES - 1
+        for half in range(2):
+            for og in range(OUT_GROUPS):
+                ready.extend([(tau, og, k_pass) for k_pass in HALVES[half]])
+        advance(tail_pool, len(ready))

@@ -26,10 +26,10 @@ WORDS = K_PASS // 2
 SPLINE_PASSES = 8
 BASE_PASS = SPLINE_PASSES
 PASSES = SPLINE_PASSES + 1
-PASS_ORDER = (0, 1, 2, 3, 4, 5, 6, 7, BASE_PASS)
+PASS_ORDER = (BASE_PASS, 0, 1, 2, 3, 4, 5, 6, 7)
 HALF_PASSES = 4
 PASSES_BETWEEN = 5
-HALVES = (PASS_ORDER[:HALF_PASSES], PASS_ORDER[HALF_PASSES:])
+HALVES = (PASS_ORDER[: 1 + HALF_PASSES], PASS_ORDER[1 + HALF_PASSES :])
 DELIVERY_AFTER = 2
 
 X_LIMIT = 4.0
@@ -55,7 +55,7 @@ def tile_generatorhead_pb_kernel(tc, h_norm, base_w2, spline_w2, out):
         keep = ctx.enter_context(tc.tile_pool(name="keep", bufs=1))
         raw_pool = ctx.enter_context(tc.tile_pool(name="raw", bufs=4))
         grouped_pool = ctx.enter_context(tc.tile_pool(name="grouped", bufs=3))
-        result_pool = ctx.enter_context(tc.tile_pool(name="result", bufs=3))
+        result_pool = ctx.enter_context(tc.tile_pool(name="result", bufs=5))
         route_pool = ctx.enter_context(tc.psum_pool(name="routed", bufs=1))
 
         w_codes = keep.tile([P, PASSES * OUTPUTS], U32, align_bytes=64)
@@ -107,17 +107,6 @@ def tile_generatorhead_pb_kernel(tc, h_norm, base_w2, spline_w2, out):
                     scalar=4.0 * g - 2.0, op=ALU.mult,
                 )
 
-        def load_base(og):
-            blocks = raw_pool.tile([P, OUT_GROUP // 16, 64], BF16, tag="raw_base", bufs=OUT_GROUPS, align_bytes=64)
-            rows = base_w2[og * OUT_GROUP : (og + 1) * OUT_GROUP, :]
-            for q in range(4):
-                for u in range(2):
-                    nc.gpsimd.dma_start(
-                        out=blocks[32 * q + u : 32 * (q + 1) : 2],
-                        in_=rows[:, 64 * (4 * u + q) : 64 * (4 * u + q + 1)].rearrange("(j o) k -> o j k", o=16),
-                    )
-            return blocks
-
         def transpose_words(bank, words, h):
             for t in range(2):
                 for u in range(2):
@@ -127,218 +116,218 @@ def tile_generatorhead_pb_kernel(tc, h_norm, base_w2, spline_w2, out):
                         identity=ident_f32[:],
                     )
 
-        with tc.psum_pool(name="bank", bufs=4) as bank_pool:
-            with tc.psum_pool(name="prep_bank", bufs=3) as prep_bank:
-                x_tok = raw_pool.tile([P, TOKEN_TILES, FEATURES], BF16, tag="raw")
-                nc.sync.dma_start(out=x_tok[:], in_=x_rows)
-                raw_base = [load_base(og) for og in range(OUT_GROUPS)]
+        with tc.psum_pool(name="prep_bank", bufs=3) as prep_bank:
+            x_tok = raw_pool.tile([P, TOKEN_TILES, FEATURES], BF16, tag="raw_base", bufs=2)
+            nc.sync.dma_start(out=x_tok[:], in_=x_rows)
 
-                silu_grouped = grouped_pool.tile([P, 4 * TOKENS], BF16, tag="grouped", align_bytes=64)
-                silu_view = silu_grouped[:].rearrange("p (h n u e) -> p h n u e", h=2, u=2, e=2)
-                for h in range(2):
-                    bank = prep_bank.tile([P, 2, 2 * P], F32, tag="prep")
-                    transpose_words(bank, x_tok[:].bitcast(F32), h)
-                    nc.scalar.activation(
-                        out=silu_view[:, h],
-                        in_=bank[:].bitcast(BF16).rearrange("p u (n e) -> p n u e", e=2),
-                        func=ACT.Silu,
-                    )
-                x_twice = raw_pool.tile([P, TOKEN_TILES * FEATURES // P, 2, P], BF16, tag="raw")
-                x_split = x_tok[:].rearrange("p t (G r u f) -> p u (t G) r f", r=2, u=2, f=32)
-                twice_split = x_twice[:].rearrange("p j u (r b f) -> p u b j r f", r=2, b=2)
-                for u in range(2):
-                    for b in range(2):
-                        nc.vector.tensor_scalar(
-                            out=twice_split[:, u, b], in0=x_split[:, u],
-                            scalar1=-X_LIMIT, scalar2=X_LIMIT, op0=ALU.max, op1=ALU.min,
-                        )
-
-                for pair in range(SPLINE_PASSES // 2):
-                    flipped = prep_bank.tile([P, 2, TOKENS], BF16, tag="prep")
-                    for u in range(2):
-                        for tau in range(TOKEN_TILES):
-                            nc.tensor.transpose(
-                                out=flipped[:, u, tau * P : (tau + 1) * P],
-                                in_=x_twice[:, tau * (FEATURES // P) + pair, u, :],
-                                identity=ident_bf16[:],
-                            )
-                    nc.vector.tensor_copy(out=x_rep[:, pair], in_=flipped[:])
-
-                base_col = act_column(0, BASE_PASS)
-                nc.vector.quantize_mx(
-                    out=act_codes[:, base_col : base_col + TOKENS].bitcast(FP8X4),
-                    scales=act_scales[:, base_col : base_col + TOKENS],
-                    in_=silu_grouped[:],
+            silu_grouped = grouped_pool.tile([P, 4 * TOKENS], BF16, tag="grouped", align_bytes=64)
+            silu_view = silu_grouped[:].rearrange("p (h n u e) -> p h n u e", h=2, u=2, e=2)
+            for h in range(2):
+                bank = prep_bank.tile([P, 2, 2 * P], F32, tag="prep")
+                transpose_words(bank, x_tok[:].bitcast(F32), h)
+                nc.scalar.activation(
+                    out=silu_view[:, h],
+                    in_=bank[:].bitcast(BF16).rearrange("p u (n e) -> p n u e", e=2),
+                    func=ACT.Silu,
                 )
-
-            work = ctx.enter_context(tc.tile_pool(name="work", bufs=2))
-
-            def evaluate_chunk(tau, g0, n_passes):
-                chunk = n_passes * P
-                x_here = x_rep[:, g0 // 2 : (g0 + n_passes) // 2, :, tau * P : (tau + 1) * P].rearrange("p g u t -> p g t u")
-                away = work.tile([P, 2, chunk], F32, tag="away")
-                for e in range(2):
-                    nc.scalar.activation(
-                        out=away[:, e, :].rearrange("p (g t u) -> p g t u", t=P, u=2), in_=x_here,
-                        func=ACT.Abs, scale=2.5, bias=z_centre[:, e : e + 1],
-                    )
-                minus_two = two_col[:, 0:1]
-                hat = work.tile([P, 2, chunk], F32, tag="hat")
-                nc.scalar.activation(out=hat[:], in_=away[:], func=ACT.Abs, scale=1.0, bias=minus_two)
-                inner = work.tile([P, 2, chunk], F32, tag="inner")
-                nc.scalar.activation(out=inner[:], in_=away[:], func=ACT.Square, scale=ROOT_HALF, bias=two_col[:, 1:2])
-                nc.vector.tensor_scalar(out=hat[:], in0=hat[:], scalar1=2.0, scalar2=-2.0, op0=ALU.min, op1=ALU.add)
-                outer = work.tile([P, 2, chunk], F32, tag="outer")
-                nc.scalar.activation(out=outer[:], in_=hat[:], func=ACT.Square, scale=ROOT_SIXTH)
-                side = work.tile([P, chunk, 2], BF16, tag="side")
-                for e in range(2):
+            x_twice = raw_pool.tile([P, TOKEN_TILES * FEATURES // P, 2, P], BF16, tag="raw")
+            x_split = x_tok[:].rearrange("p t (G r u f) -> p u (t G) r f", r=2, u=2, f=32)
+            twice_split = x_twice[:].rearrange("p j u (r b f) -> p u b j r f", r=2, b=2)
+            for u in range(2):
+                for b in range(2):
                     nc.vector.tensor_scalar(
-                        out=side[:, :, e].rearrange("p (g t u) -> p g t u", t=P, u=2), in0=x_here,
-                        scalar1=border[:, e : e + 1], scalar2=0.5, op0=ALU.is_ge, op1=ALU.subtract,
+                        out=twice_split[:, u, b], in0=x_split[:, u],
+                        scalar1=-X_LIMIT, scalar2=X_LIMIT, op0=ALU.max, op1=ALU.min,
                     )
-                nc.vector.tensor_tensor(out=inner[:], in0=hat[:], in1=inner[:], op=ALU.mult)
-                nc.vector.scalar_tensor_tensor(
-                    out=outer[:], in0=hat[:], scalar=-1.0, in1=outer[:], op0=ALU.mult, op1=ALU.mult,
-                )
-                signed = work.tile([P, chunk, 2], BF16, tag="signed")
-                nc.vector.scalar_tensor_tensor(
-                    out=signed[:], in0=inner[:].rearrange("p e j -> p j e"), scalar=2.0 / 3.0,
-                    in1=outer[:].rearrange("p e j -> p j e"), op0=ALU.add, op1=ALU.min,
-                )
-                nc.vector.tensor_tensor(out=signed[:], in0=signed[:], in1=side[:], op=ALU.mult)
-                return signed
 
-            def deliver_chunk(signed, tau, g0, n_passes):
-                values = work.tile([P, n_passes * 4 * P], BF16, tag="values", align_bytes=64)
-                for pair in range(n_passes // 2):
-                    routed = route_pool.tile([P, 2, 4 * P], BF16, tag="routed")
-                    for r in range(2):
-                        nc.tensor.matmul(
-                            out=routed[:, r, :],
-                            lhsT=route[:, r, :],
-                            rhs=signed[:, pair * 2 * P : (pair + 1) * 2 * P, :].rearrange("p j e -> p (j e)"),
-                            start=True, stop=True,
+            for pair in range(SPLINE_PASSES // 2):
+                flipped = prep_bank.tile([P, 2, TOKENS], BF16, tag="prep")
+                for u in range(2):
+                    for tau in range(TOKEN_TILES):
+                        nc.tensor.transpose(
+                            out=flipped[:, u, tau * P : (tau + 1) * P],
+                            in_=x_twice[:, tau * (FEATURES // P) + pair, u, :],
+                            identity=ident_bf16[:],
                         )
+                nc.vector.tensor_copy(out=x_rep[:, pair], in_=flipped[:])
+
+            base_col = act_column(0, BASE_PASS)
+            nc.vector.quantize_mx(
+                out=act_codes[:, base_col : base_col + TOKENS].bitcast(FP8X4),
+                scales=act_scales[:, base_col : base_col + TOKENS],
+                in_=silu_grouped[:],
+            )
+
+        work = ctx.enter_context(tc.tile_pool(name="work", bufs=2))
+
+        def evaluate_chunk(tau, g0, n_passes):
+            chunk = n_passes * P
+            x_here = x_rep[:, g0 // 2 : (g0 + n_passes) // 2, :, tau * P : (tau + 1) * P].rearrange("p g u t -> p g t u")
+            away = work.tile([P, 2, chunk], F32, tag="away")
+            for e in range(2):
+                nc.scalar.activation(
+                    out=away[:, e, :].rearrange("p (g t u) -> p g t u", t=P, u=2), in_=x_here,
+                    func=ACT.Abs, scale=2.5, bias=z_centre[:, e : e + 1],
+                )
+            minus_two = two_col[:, 0:1]
+            hat = work.tile([P, 2, chunk], F32, tag="hat")
+            nc.scalar.activation(out=hat[:], in_=away[:], func=ACT.Abs, scale=1.0, bias=minus_two)
+            inner = work.tile([P, 2, chunk], F32, tag="inner")
+            nc.scalar.activation(out=inner[:], in_=away[:], func=ACT.Square, scale=ROOT_HALF, bias=two_col[:, 1:2])
+            nc.vector.tensor_scalar(out=hat[:], in0=hat[:], scalar1=2.0, scalar2=-2.0, op0=ALU.min, op1=ALU.add)
+            outer = work.tile([P, 2, chunk], F32, tag="outer")
+            nc.scalar.activation(out=outer[:], in_=hat[:], func=ACT.Square, scale=ROOT_SIXTH)
+            side = work.tile([P, chunk, 2], BF16, tag="side")
+            for e in range(2):
+                nc.vector.tensor_scalar(
+                    out=side[:, :, e].rearrange("p (g t u) -> p g t u", t=P, u=2), in0=x_here,
+                    scalar1=border[:, e : e + 1], scalar2=0.5, op0=ALU.is_ge, op1=ALU.subtract,
+                )
+            nc.vector.tensor_tensor(out=inner[:], in0=hat[:], in1=inner[:], op=ALU.mult)
+            nc.vector.scalar_tensor_tensor(
+                out=outer[:], in0=hat[:], scalar=-1.0, in1=outer[:], op0=ALU.mult, op1=ALU.mult,
+            )
+            signed = work.tile([P, chunk, 2], BF16, tag="signed")
+            nc.vector.scalar_tensor_tensor(
+                out=signed[:], in0=inner[:].rearrange("p e j -> p j e"), scalar=2.0 / 3.0,
+                in1=outer[:].rearrange("p e j -> p j e"), op0=ALU.add, op1=ALU.min,
+            )
+            nc.vector.tensor_tensor(out=signed[:], in0=signed[:], in1=side[:], op=ALU.mult)
+            return signed
+
+        def deliver_chunk(signed, tau, g0, n_passes):
+            values = work.tile([P, n_passes * 4 * P], BF16, tag="values", align_bytes=64)
+            for pair in range(n_passes // 2):
+                routed = route_pool.tile([P, 2, 4 * P], BF16, tag="routed")
+                for r in range(2):
+                    nc.tensor.matmul(
+                        out=routed[:, r, :],
+                        lhsT=route[:, r, :],
+                        rhs=signed[:, pair * 2 * P : (pair + 1) * 2 * P, :].rearrange("p j e -> p (j e)"),
+                        start=True, stop=True,
+                    )
+                split = values[:, pair * 8 * P : (pair + 1) * 8 * P]
+                if pair == 0:
                     nc.vector.tensor_single_scalar(
-                        out=values[:, pair * 8 * P : (pair + 1) * 8 * P], in_=routed[:].rearrange("p r j -> p (r j)"),
-                        scalar=0.0, op=ALU.max,
+                        out=split, in_=routed[:].rearrange("p r j -> p (r j)"), scalar=0.0, op=ALU.max,
                     )
-                col = act_column(tau, g0)
-                nc.vector.quantize_mx(
-                    out=act_codes[:, col : col + n_passes * P].bitcast(FP8X4),
-                    scales=act_scales[:, col : col + n_passes * P],
-                    in_=values[:],
-                )
+                else:
+                    nc.scalar.activation(out=split, in_=routed[:].rearrange("p r j -> p (r j)"), func=ACT.Relu)
+            col = act_column(tau, g0)
+            nc.vector.quantize_mx(
+                out=act_codes[:, col : col + n_passes * P].bitcast(FP8X4),
+                scales=act_scales[:, col : col + n_passes * P],
+                in_=values[:],
+            )
 
-            def quantise_weight_pass(words, k_pass, og):
-                grouped = grouped_pool.tile([P, 4 * OUT_GROUP], BF16, tag="grouped", align_bytes=64)
-                grouped_words = grouped[:].bitcast(F32).rearrange("p (h n u) -> p h n u", h=2, u=2)
-                for h in range(2):
-                    bank = bank_pool.tile([P, 2, 2 * P], F32, tag="bank")
-                    transpose_words(bank, words, h)
-                    if og == 0 and k_pass < HALF_PASSES and h == 1:
-                        nc.vector.tensor_copy(out=grouped_words[:, h], in_=bank[:].rearrange("p u n -> p n u"))
-                    else:
-                        nc.scalar.copy(out=grouped_words[:, h], in_=bank[:].rearrange("p u n -> p n u"))
-                quantise_grouped(grouped, k_pass, og)
+        def quantise_weight_pass(words, k_pass, og):
+            grouped = grouped_pool.tile([P, 4 * OUT_GROUP], BF16, tag="grouped", align_bytes=64)
+            grouped_words = grouped[:].bitcast(F32).rearrange("p (h n u) -> p h n u", h=2, u=2)
+            for h in range(2):
+                bank = bank_pool.tile([P, 2, 2 * P], F32, tag="bank")
+                transpose_words(bank, words, h)
+                if og == 0 and k_pass in HALVES[0] and h == 1:
+                    nc.vector.tensor_copy(out=grouped_words[:, h], in_=bank[:].rearrange("p u n -> p n u"))
+                else:
+                    nc.scalar.copy(out=grouped_words[:, h], in_=bank[:].rearrange("p u n -> p n u"))
+            quantise_grouped(grouped, k_pass, og)
 
-            def quantise_grouped(grouped, k_pass, og):
-                col = k_pass * OUTPUTS + og * OUT_GROUP
-                nc.vector.quantize_mx(
-                    out=w_codes[:, col : col + OUT_GROUP].bitcast(FP8X4),
-                    scales=w_scales[:, col : col + OUT_GROUP],
-                    in_=grouped[:],
-                )
+        def quantise_grouped(grouped, k_pass, og):
+            col = k_pass * OUTPUTS + og * OUT_GROUP
+            nc.vector.quantize_mx(
+                out=w_codes[:, col : col + OUT_GROUP].bitcast(FP8X4),
+                scales=w_scales[:, col : col + OUT_GROUP],
+                in_=grouped[:],
+            )
 
-            def quantise_base_pass(og):
-                grouped = grouped_pool.tile([P, 4 * OUT_GROUP], BF16, tag="grouped", align_bytes=64)
-                nc.vector.transpose(
-                    out=grouped[:].bitcast(F32),
-                    in_=raw_base[og][:].rearrange("p j k -> p (j k)").bitcast(F32),
-                )
-                quantise_grouped(grouped, BASE_PASS, og)
-
-            def weights(og, half, after_a_pass):
-                rows = slice(og * OUT_GROUP, (og + 1) * OUT_GROUP)
-                for pair_of_passes in range(half * HALF_PASSES // 2, (half + 1) * HALF_PASSES // 2):
-                    raw = raw_pool.tile([P, ROW_TILES, 2 * K_PASS], BF16, tag="raw")
-                    cols = slice(pair_of_passes * 2 * K_PASS, (pair_of_passes + 1) * 2 * K_PASS)
-                    nc.sync.dma_start(out=raw[:], in_=spline_rows[rows, cols].rearrange("(t p) k -> p t k", p=P))
-                    for q in range(2):
-                        quantise_weight_pass(
-                            raw[:].bitcast(F32)[:, :, q * WORDS : (q + 1) * WORDS], 2 * pair_of_passes + q, og
-                        )
-                        after_a_pass()
-                if half == 1:
-                    quantise_base_pass(og)
+        def weights(og, half, after_a_pass):
+            rows = slice(og * OUT_GROUP, (og + 1) * OUT_GROUP)
+            if half == 0:
+                raw_base = raw_pool.tile([P, ROW_TILES, K_PASS], BF16, tag="raw_base", bufs=2)
+                nc.sync.dma_start(out=raw_base[:], in_=base_w2[rows, :].rearrange("(t p) k -> p t k", p=P))
+                quantise_weight_pass(raw_base[:].bitcast(F32), BASE_PASS, og)
+                after_a_pass()
+            for pair_of_passes in range(half * HALF_PASSES // 2, (half + 1) * HALF_PASSES // 2):
+                raw = raw_pool.tile([P, ROW_TILES, 2 * K_PASS], BF16, tag="raw")
+                cols = slice(pair_of_passes * 2 * K_PASS, (pair_of_passes + 1) * 2 * K_PASS)
+                nc.sync.dma_start(out=raw[:], in_=spline_rows[rows, cols].rearrange("(t p) k -> p t k", p=P))
+                for q in range(2):
+                    quantise_weight_pass(
+                        raw[:].bitcast(F32)[:, :, q * WORDS : (q + 1) * WORDS], 2 * pair_of_passes + q, og
+                    )
                     after_a_pass()
 
-            def multiply(acc, tau, og, passes):
-                for k_pass in passes:
-                    a_col = act_column(tau, k_pass)
-                    w_col = k_pass * OUTPUTS + og * OUT_GROUP
-                    nc.tensor.matmul_mx(
-                        out=acc[:],
-                        lhsT=act_codes[:, a_col : a_col + P].bitcast(FP8X4),
-                        lhsT_scale=act_scales[:, a_col : a_col + P],
-                        rhs=w_codes[:, w_col : w_col + OUT_GROUP].bitcast(FP8X4),
-                        rhs_scale=w_scales[:, w_col : w_col + OUT_GROUP],
-                        start=(k_pass == PASS_ORDER[0]),
-                        stop=(k_pass == PASS_ORDER[-1]),
-                    )
+        def multiply(acc, tau, og, passes):
+            for k_pass in passes:
+                a_col = act_column(tau, k_pass)
+                w_col = k_pass * OUTPUTS + og * OUT_GROUP
+                nc.tensor.matmul_mx(
+                    out=acc[:],
+                    lhsT=act_codes[:, a_col : a_col + P].bitcast(FP8X4),
+                    lhsT_scale=act_scales[:, a_col : a_col + P],
+                    rhs=w_codes[:, w_col : w_col + OUT_GROUP].bitcast(FP8X4),
+                    rhs_scale=w_scales[:, w_col : w_col + OUT_GROUP],
+                    start=(k_pass == PASS_ORDER[0]),
+                    stop=(k_pass == PASS_ORDER[-1]),
+                )
 
-            def store(acc, tau, og):
-                result = result_pool.tile([P, OUT_GROUP], F32, tag="result")
+        def store(acc, tau, og):
+            result = result_pool.tile([P, OUT_GROUP], F32, tag="result")
+            if og % 2 == 0:
+                nc.vector.tensor_copy(out=result[:], in_=acc[:])
+            else:
                 nc.scalar.copy(out=result[:], in_=acc[:])
-                nc.sync.dma_start(out=out[tau, :, og * OUT_GROUP : (og + 1) * OUT_GROUP], in_=result[:])
+            nc.sync.dma_start(out=out[tau, :, og * OUT_GROUP : (og + 1) * OUT_GROUP], in_=result[:])
 
-            accs = {}
-            ready = []
-            begun = []
-            evaluated = []
-            turns = []
+        accs = {}
+        ready = []
+        begun = []
+        evaluated = []
+        turns = []
 
-            def advance(pool, passes):
-                for tau, og, k_pass in ready[len(begun) : len(begun) + passes]:
-                    if k_pass == PASS_ORDER[0]:
-                        acc = pool.tile([P, OUT_GROUP], F32, tag="acc")
-                        accs[tau, og] = acc
-                    multiply(accs[tau, og], tau, og, (k_pass,))
-                    begun.append(k_pass)
-                    if k_pass == PASS_ORDER[-1]:
-                        store(accs[tau, og], tau, og)
+        def multiply_passes(pool, passes):
+            for tau, og, k_pass in passes:
+                if k_pass == PASS_ORDER[0]:
+                    acc = pool.tile([P, OUT_GROUP], F32, tag="acc")
+                    accs[tau, og] = acc
+                multiply(accs[tau, og], tau, og, (k_pass,))
+                if k_pass == PASS_ORDER[-1]:
+                    store(accs[tau, og], tau, og)
 
-            def deliver():
-                for chunk in evaluated:
-                    deliver_chunk(*chunk)
-                    tau, half = chunk[1], chunk[2] // HALF_PASSES
-                    if half == 1 and tau < TOKEN_TILES - 1:
-                        for og in range(tau + 1):
-                            ready.extend([(tau, og, k_pass) for k_pass in PASS_ORDER])
-                evaluated.clear()
+        def deliver():
+            for chunk in evaluated:
+                deliver_chunk(*chunk)
+                tau, half = chunk[1], chunk[2] // HALF_PASSES
+                if half == 1 and tau < TOKEN_TILES - 1:
+                    for og in range(tau + 1):
+                        ready.extend([(tau, og, k_pass) for k_pass in PASS_ORDER])
+            evaluated.clear()
 
-            with tc.psum_pool(name="acc", bufs=3) as acc_pool:
+        acc_pool = ctx.enter_context(tc.psum_pool(name="acc", bufs=3))
+        with tc.psum_pool(name="bank", bufs=4) as bank_pool:
 
-                def after_a_weight_pass():
-                    turns.append(1)
-                    if len(turns) == DELIVERY_AFTER:
-                        deliver()
-                    advance(acc_pool, PASSES_BETWEEN)
+            def after_a_weight_pass():
+                turns.append(1)
+                if len(turns) == DELIVERY_AFTER:
+                    deliver()
+                passes = ready[len(begun) : len(begun) + PASSES_BETWEEN]
+                multiply_passes(acc_pool, passes)
+                begun.extend(passes)
 
-                for step in range(2 * TOKEN_TILES):
-                    last, half = divmod(step, 2)
-                    weights(last, half, after_a_weight_pass)
-                    for tau in range(last):
-                        ready.extend([(tau, last, k_pass) for k_pass in HALVES[half]])
-                    signed = evaluate_chunk(last, half * HALF_PASSES, HALF_PASSES)
-                    evaluated.append((signed, last, half * HALF_PASSES, HALF_PASSES))
-                    turns.clear()
-                deliver()
-                advance(acc_pool, len(ready))
+            for step in range(2 * TOKEN_TILES):
+                last, half = divmod(step, 2)
+                weights(last, half, after_a_weight_pass)
+                for tau in range(last):
+                    ready.extend([(tau, last, k_pass) for k_pass in HALVES[half]])
+                signed = evaluate_chunk(last, half * HALF_PASSES, HALF_PASSES)
+                evaluated.append((signed, last, half * HALF_PASSES, HALF_PASSES))
+                turns.clear()
 
+        deliver()
         tail_pool = ctx.enter_context(tc.psum_pool(name="tail", bufs=4))
-        tau = TOKEN_TILES - 1
-        for half in range(2):
-            for og in range(OUT_GROUPS):
-                ready.extend([(tau, og, k_pass) for k_pass in HALVES[half]])
-        advance(tail_pool, len(ready))
+        last_tile = [[[(TOKEN_TILES - 1, og, k_pass) for k_pass in HALVES[half]] for og in range(OUT_GROUPS)] for half in range(2)]
+        for passes in last_tile[0][:-1]:
+            multiply_passes(tail_pool, passes)
+        multiply_passes(acc_pool, ready[len(begun) :])
+        for passes in last_tile[0][-1:] + last_tile[1]:
+            multiply_passes(tail_pool, passes)

import math
from contextlib import ExitStack

import concourse.mybir as mybir
from concourse.masks import make_identity

F32 = mybir.dt.float32
BF16 = mybir.dt.bfloat16
I32 = mybir.dt.int32
U32 = mybir.dt.uint32
U8 = mybir.dt.uint8
FP8X4 = mybir.dt.float8_e4m3fn_x4
ACT = mybir.ActivationFunctionType
ALU = mybir.AluOpType

P = 128
TOKEN_TILES = 4
TOKENS = TOKEN_TILES * P
FEATURES = 512
OUTPUTS = 2048
OUT_GROUP = 512
OUT_GROUPS = OUTPUTS // OUT_GROUP
ROW_TILES = OUT_GROUP // P
K_PASS = 512
WORDS = K_PASS // 2
SPLINE_PASSES = 8
BASE_PASS = SPLINE_PASSES
PASSES = SPLINE_PASSES + 1
PASS_ORDER = (BASE_PASS, 0, 1, 2, 3, 4, 5, 6, 7)
HALF_PASSES = 4
PASSES_BETWEEN = 5
HALVES = (PASS_ORDER[: 1 + HALF_PASSES], PASS_ORDER[1 + HALF_PASSES :])
DELIVERY_AFTER = 2

X_LIMIT = 4.0
ROOT_SIXTH = math.sqrt(1.0 / 6.0)
ROOT_HALF = math.sqrt(0.5)
ROOT_TWO = math.sqrt(2.0)

FLOPS = 2 * TOKENS * OUTPUTS * (FEATURES + 8 * FEATURES)


def act_column(tau, k_pass):
    if k_pass == BASE_PASS:
        return SPLINE_PASSES * TOKENS + tau * P
    return (tau * SPLINE_PASSES + k_pass) * P


def tile_generatorhead_pb_kernel(tc, h_norm, base_w2, spline_w2, out):
    nc = tc.nc
    x_rows = h_norm.rearrange("b s f -> s b f")
    spline_rows = spline_w2.rearrange("o i c -> o (i c)")

    with ExitStack() as ctx:
        keep = ctx.enter_context(tc.tile_pool(name="keep", bufs=1))
        raw_pool = ctx.enter_context(tc.tile_pool(name="raw", bufs=4))
        grouped_pool = ctx.enter_context(tc.tile_pool(name="grouped", bufs=3))
        result_pool = ctx.enter_context(tc.tile_pool(name="result", bufs=5))
        route_pool = ctx.enter_context(tc.psum_pool(name="routed", bufs=1))

        w_codes = keep.tile([P, PASSES * OUTPUTS], U32, align_bytes=64)
        w_scales = keep.tile([P, PASSES * OUTPUTS], U8, align_bytes=64)
        act_codes = keep.tile([P, PASSES * TOKENS], U32, align_bytes=64)
        act_scales = keep.tile([P, PASSES * TOKENS], U8, align_bytes=64)
        x_rep = keep.tile([P, SPLINE_PASSES // 2, 2, TOKENS], BF16)

        ident_f32 = keep.tile([P, P], F32)
        make_identity(nc, ident_f32[:])
        ident_bf16 = keep.tile([P, P], BF16)
        make_identity(nc, ident_bf16[:])

        lane = keep.tile([P, 1], I32)
        nc.gpsimd.iota(out=lane[:], pattern=[[0, 1]], base=0, channel_multiplier=1)
        lane_mod2 = keep.tile([P, 1], I32)
        nc.vector.tensor_single_scalar(out=lane_mod2[:], in_=lane[:], scalar=32, op=ALU.bitwise_and)
        half32 = keep.tile([P, 1], F32)
        nc.vector.tensor_copy(out=half32[:], in_=lane_mod2[:])
        half = keep.tile([P, 1], F32)
        nc.vector.tensor_single_scalar(out=half[:], in_=half32[:], scalar=1.0 / 32.0, op=ALU.mult)
        z_centre = keep.tile([P, 2], F32)
        border = keep.tile([P, 2], F32)
        for e in range(2):
            nc.vector.tensor_scalar(
                out=z_centre[:, e : e + 1], in0=half[:],
                scalar1=-2.0, scalar2=1.5 - e, op0=ALU.mult, op1=ALU.add,
            )
            nc.vector.tensor_scalar(
                out=border[:, e : e + 1], in0=half[:],
                scalar1=2.0 / 2.5, scalar2=(e - 1.5) / 2.5, op0=ALU.mult, op1=ALU.add,
            )

        two_col = keep.tile([P, 2], F32)
        nc.vector.tensor_scalar(
            out=two_col[:, 0:1], in0=half[:], scalar1=0.0, scalar2=-2.0, op0=ALU.mult, op1=ALU.add,
        )
        nc.vector.tensor_scalar(
            out=two_col[:, 1:2], in0=half[:], scalar1=0.0, scalar2=-ROOT_TWO, op0=ALU.mult, op1=ALU.add,
        )

        route = keep.tile([P, 2, P], BF16)
        nc.vector.memset(route[:], 0.0)
        for h in range(2):
            for g in range(2):
                nc.vector.tensor_single_scalar(
                    out=route[:, h, :].rearrange("p (f g b) -> p g f b", g=2, b=2)[:, g],
                    in_=ident_bf16[:, h * (P // 2) : (h + 1) * (P // 2)].rearrange("p (b f) -> p f b", b=2),
                    scalar=4.0 * g - 2.0, op=ALU.mult,
                )

        def transpose_words(bank, words, h):
            for t in range(2):
                for u in range(2):
                    nc.tensor.transpose(
                        out=bank[:, u, t * P : (t + 1) * P],
                        in_=words[:, 2 * h + t, u * P : (u + 1) * P],
                        identity=ident_f32[:],
                    )

        with tc.psum_pool(name="prep_bank", bufs=3) as prep_bank:
            x_tok = raw_pool.tile([P, TOKEN_TILES, FEATURES], BF16, tag="raw_base", bufs=2)
            nc.sync.dma_start(out=x_tok[:], in_=x_rows)

            silu_grouped = grouped_pool.tile([P, 4 * TOKENS], BF16, tag="grouped", align_bytes=64)
            silu_view = silu_grouped[:].rearrange("p (h n u e) -> p h n u e", h=2, u=2, e=2)
            for h in range(2):
                bank = prep_bank.tile([P, 2, 2 * P], F32, tag="prep")
                transpose_words(bank, x_tok[:].bitcast(F32), h)
                nc.scalar.activation(
                    out=silu_view[:, h],
                    in_=bank[:].bitcast(BF16).rearrange("p u (n e) -> p n u e", e=2),
                    func=ACT.Silu,
                )
            x_twice = raw_pool.tile([P, TOKEN_TILES * FEATURES // P, 2, P], BF16, tag="raw")
            x_split = x_tok[:].rearrange("p t (G r u f) -> p u (t G) r f", r=2, u=2, f=32)
            twice_split = x_twice[:].rearrange("p j u (r b f) -> p u b j r f", r=2, b=2)
            for u in range(2):
                for b in range(2):
                    nc.vector.tensor_scalar(
                        out=twice_split[:, u, b], in0=x_split[:, u],
                        scalar1=-X_LIMIT, scalar2=X_LIMIT, op0=ALU.max, op1=ALU.min,
                    )

            for pair in range(SPLINE_PASSES // 2):
                flipped = prep_bank.tile([P, 2, TOKENS], BF16, tag="prep")
                for u in range(2):
                    for tau in range(TOKEN_TILES):
                        nc.tensor.transpose(
                            out=flipped[:, u, tau * P : (tau + 1) * P],
                            in_=x_twice[:, tau * (FEATURES // P) + pair, u, :],
                            identity=ident_bf16[:],
                        )
                nc.vector.tensor_copy(out=x_rep[:, pair], in_=flipped[:])

            base_col = act_column(0, BASE_PASS)
            nc.vector.quantize_mx(
                out=act_codes[:, base_col : base_col + TOKENS].bitcast(FP8X4),
                scales=act_scales[:, base_col : base_col + TOKENS],
                in_=silu_grouped[:],
            )

        work = ctx.enter_context(tc.tile_pool(name="work", bufs=2))

        def evaluate_chunk(tau, g0, n_passes):
            chunk = n_passes * P
            x_here = x_rep[:, g0 // 2 : (g0 + n_passes) // 2, :, tau * P : (tau + 1) * P].rearrange("p g u t -> p g t u")
            away = work.tile([P, 2, chunk], F32, tag="away")
            for e in range(2):
                nc.scalar.activation(
                    out=away[:, e, :].rearrange("p (g t u) -> p g t u", t=P, u=2), in_=x_here,
                    func=ACT.Abs, scale=2.5, bias=z_centre[:, e : e + 1],
                )
            minus_two = two_col[:, 0:1]
            hat = work.tile([P, 2, chunk], F32, tag="hat")
            nc.scalar.activation(out=hat[:], in_=away[:], func=ACT.Abs, scale=1.0, bias=minus_two)
            inner = work.tile([P, 2, chunk], F32, tag="inner")
            nc.scalar.activation(out=inner[:], in_=away[:], func=ACT.Square, scale=ROOT_HALF, bias=two_col[:, 1:2])
            nc.vector.tensor_scalar(out=hat[:], in0=hat[:], scalar1=2.0, scalar2=-2.0, op0=ALU.min, op1=ALU.add)
            outer = work.tile([P, 2, chunk], F32, tag="outer")
            nc.scalar.activation(out=outer[:], in_=hat[:], func=ACT.Square, scale=ROOT_SIXTH)
            side = work.tile([P, chunk, 2], BF16, tag="side")
            for e in range(2):
                nc.vector.tensor_scalar(
                    out=side[:, :, e].rearrange("p (g t u) -> p g t u", t=P, u=2), in0=x_here,
                    scalar1=border[:, e : e + 1], scalar2=0.5, op0=ALU.is_ge, op1=ALU.subtract,
                )
            nc.vector.tensor_tensor(out=inner[:], in0=hat[:], in1=inner[:], op=ALU.mult)
            nc.vector.scalar_tensor_tensor(
                out=outer[:], in0=hat[:], scalar=-1.0, in1=outer[:], op0=ALU.mult, op1=ALU.mult,
            )
            signed = work.tile([P, chunk, 2], BF16, tag="signed")
            nc.vector.scalar_tensor_tensor(
                out=signed[:], in0=inner[:].rearrange("p e j -> p j e"), scalar=2.0 / 3.0,
                in1=outer[:].rearrange("p e j -> p j e"), op0=ALU.add, op1=ALU.min,
            )
            nc.vector.tensor_tensor(out=signed[:], in0=signed[:], in1=side[:], op=ALU.mult)
            return signed

        def deliver_chunk(signed, tau, g0, n_passes):
            values = work.tile([P, n_passes * 4 * P], BF16, tag="values", align_bytes=64)
            for pair in range(n_passes // 2):
                routed = route_pool.tile([P, 2, 4 * P], BF16, tag="routed")
                for r in range(2):
                    nc.tensor.matmul(
                        out=routed[:, r, :],
                        lhsT=route[:, r, :],
                        rhs=signed[:, pair * 2 * P : (pair + 1) * 2 * P, :].rearrange("p j e -> p (j e)"),
                        start=True, stop=True,
                    )
                split = values[:, pair * 8 * P : (pair + 1) * 8 * P]
                if pair == 0:
                    nc.vector.tensor_single_scalar(
                        out=split, in_=routed[:].rearrange("p r j -> p (r j)"), scalar=0.0, op=ALU.max,
                    )
                else:
                    nc.scalar.activation(out=split, in_=routed[:].rearrange("p r j -> p (r j)"), func=ACT.Relu)
            col = act_column(tau, g0)
            nc.vector.quantize_mx(
                out=act_codes[:, col : col + n_passes * P].bitcast(FP8X4),
                scales=act_scales[:, col : col + n_passes * P],
                in_=values[:],
            )

        def quantise_weight_pass(words, k_pass, og):
            grouped = grouped_pool.tile([P, 4 * OUT_GROUP], BF16, tag="grouped", align_bytes=64)
            grouped_words = grouped[:].bitcast(F32).rearrange("p (h n u) -> p h n u", h=2, u=2)
            for h in range(2):
                bank = bank_pool.tile([P, 2, 2 * P], F32, tag="bank")
                transpose_words(bank, words, h)
                if og == 0 and k_pass in HALVES[0] and h == 1:
                    nc.vector.tensor_copy(out=grouped_words[:, h], in_=bank[:].rearrange("p u n -> p n u"))
                else:
                    nc.scalar.copy(out=grouped_words[:, h], in_=bank[:].rearrange("p u n -> p n u"))
            quantise_grouped(grouped, k_pass, og)

        def quantise_grouped(grouped, k_pass, og):
            col = k_pass * OUTPUTS + og * OUT_GROUP
            nc.vector.quantize_mx(
                out=w_codes[:, col : col + OUT_GROUP].bitcast(FP8X4),
                scales=w_scales[:, col : col + OUT_GROUP],
                in_=grouped[:],
            )

        def weights(og, half, after_a_pass):
            rows = slice(og * OUT_GROUP, (og + 1) * OUT_GROUP)
            if half == 0:
                raw_base = raw_pool.tile([P, ROW_TILES, K_PASS], BF16, tag="raw_base", bufs=2)
                nc.sync.dma_start(out=raw_base[:], in_=base_w2[rows, :].rearrange("(t p) k -> p t k", p=P))
                quantise_weight_pass(raw_base[:].bitcast(F32), BASE_PASS, og)
                after_a_pass()
            for pair_of_passes in range(half * HALF_PASSES // 2, (half + 1) * HALF_PASSES // 2):
                raw = raw_pool.tile([P, ROW_TILES, 2 * K_PASS], BF16, tag="raw")
                cols = slice(pair_of_passes * 2 * K_PASS, (pair_of_passes + 1) * 2 * K_PASS)
                nc.sync.dma_start(out=raw[:], in_=spline_rows[rows, cols].rearrange("(t p) k -> p t k", p=P))
                for q in range(2):
                    quantise_weight_pass(
                        raw[:].bitcast(F32)[:, :, q * WORDS : (q + 1) * WORDS], 2 * pair_of_passes + q, og
                    )
                    after_a_pass()

        def multiply(acc, tau, og, passes):
            for k_pass in passes:
                a_col = act_column(tau, k_pass)
                w_col = k_pass * OUTPUTS + og * OUT_GROUP
                nc.tensor.matmul_mx(
                    out=acc[:],
                    lhsT=act_codes[:, a_col : a_col + P].bitcast(FP8X4),
                    lhsT_scale=act_scales[:, a_col : a_col + P],
                    rhs=w_codes[:, w_col : w_col + OUT_GROUP].bitcast(FP8X4),
                    rhs_scale=w_scales[:, w_col : w_col + OUT_GROUP],
                    start=(k_pass == PASS_ORDER[0]),
                    stop=(k_pass == PASS_ORDER[-1]),
                )

        def store(acc, tau, og):
            result = result_pool.tile([P, OUT_GROUP], F32, tag="result")
            if og % 2 == 0:
                nc.vector.tensor_copy(out=result[:], in_=acc[:])
            else:
                nc.scalar.copy(out=result[:], in_=acc[:])
            nc.sync.dma_start(out=out[tau, :, og * OUT_GROUP : (og + 1) * OUT_GROUP], in_=result[:])

        accs = {}
        ready = []
        begun = []
        evaluated = []
        turns = []

        def multiply_passes(pool, passes):
            for tau, og, k_pass in passes:
                if k_pass == PASS_ORDER[0]:
                    acc = pool.tile([P, OUT_GROUP], F32, tag="acc")
                    accs[tau, og] = acc
                multiply(accs[tau, og], tau, og, (k_pass,))
                if k_pass == PASS_ORDER[-1]:
                    store(accs[tau, og], tau, og)

        def deliver():
            for chunk in evaluated:
                deliver_chunk(*chunk)
                tau, half = chunk[1], chunk[2] // HALF_PASSES
                if half == 1 and tau < TOKEN_TILES - 1:
                    for og in range(tau + 1):
                        ready.extend([(tau, og, k_pass) for k_pass in PASS_ORDER])
            evaluated.clear()

        acc_pool = ctx.enter_context(tc.psum_pool(name="acc", bufs=3))
        with tc.psum_pool(name="bank", bufs=4) as bank_pool:

            def after_a_weight_pass():
                turns.append(1)
                if len(turns) == DELIVERY_AFTER:
                    deliver()
                passes = ready[len(begun) : len(begun) + PASSES_BETWEEN]
                multiply_passes(acc_pool, passes)
                begun.extend(passes)

            for step in range(2 * TOKEN_TILES):
                last, half = divmod(step, 2)
                weights(last, half, after_a_weight_pass)
                for tau in range(last):
                    ready.extend([(tau, last, k_pass) for k_pass in HALVES[half]])
                signed = evaluate_chunk(last, half * HALF_PASSES, HALF_PASSES)
                evaluated.append((signed, last, half * HALF_PASSES, HALF_PASSES))
                turns.clear()

        deliver()
        tail_pool = ctx.enter_context(tc.psum_pool(name="tail", bufs=4))
        last_tile = [[[(TOKEN_TILES - 1, og, k_pass) for k_pass in HALVES[half]] for og in range(OUT_GROUPS)] for half in range(2)]
        for passes in last_tile[0][:-1]:
            multiply_passes(tail_pool, passes)
        multiply_passes(acc_pool, ready[len(begun) :])
        for passes in last_tile[0][-1:] + last_tile[1]:
            multiply_passes(tail_pool, passes)
